import numpy as np
import ml_dtypes


def mxq(x, axis, fmt="e4m3"):
    dtype, down = {"e4m3": (ml_dtypes.float8_e4m3fn, 7), "e5m2": (ml_dtypes.float8_e5m2, 14)}[fmt]
    v = np.moveaxis(np.asarray(x, np.float32).astype(ml_dtypes.bfloat16).astype(np.float64), axis, -1)
    blocks = v.reshape(v.shape[:-1] + (-1, 32))
    amax = np.abs(blocks).max(-1, keepdims=True)
    byte = np.maximum(np.where(amax > 0, np.frexp(amax)[1] - 1 + 127, 0) - down, 1)
    scale = np.exp2(byte - 127.0)
    codes = (blocks / scale).astype(np.float32).astype(dtype).astype(np.float64)
    return np.moveaxis((codes * scale).reshape(v.shape), -1, axis)


WIDE = False


def mx_kscale(k):
    if not WIDE:
        return np.ones(k)
    levels = np.array([10, -10, 5, -5, 0])
    if k % 512:
        return np.exp2(np.random.permutation(np.resize(levels, k // 32))).repeat(32)
    a = np.empty((k // 512, 16))
    for p in range(k // 512):
        a[p, :8] = np.random.permutation(np.resize(levels, 8))
        for g in range(8):
            far = levels[np.abs(levels - a[p, g]) >= 10]
            a[p, g + 8] = far[np.random.randint(len(far))]
    return np.exp2(a.ravel()).repeat(32)


BF16 = ml_dtypes.bfloat16


def bf(x):
    return np.asarray(x, np.float32).astype(BF16)


def f64(x):
    return np.asarray(x).astype(np.float64)


B, S, E, H, D, F = 2, 256, 1024, 8, 128, 4096
EPS = 1e-6
QUIET = 3e-5
GELU_C = 0.7978845608028654
HD = H * D


def rmsnorm(x, scale):
    ms = np.mean(np.square(x), axis=-1, keepdims=True)
    return x * (1.0 / np.sqrt(ms + EPS)) * scale


def gelu_tanh(v):
    return 0.5 * v * (1.0 + np.tanh(GELU_C * (v + 0.044715 * v**3)))


def setup_inputs():
    s, t = mx_kscale(HD), mx_kscale(E)
    amp = np.where(np.random.random((B, S, 1)) < 0.125, QUIET, 1.0)
    return {"attn": bf(np.random.standard_normal((B, S, H, D)) * 0.25 * amp[..., None] * s.reshape(H, D)),
            "x": bf(np.random.standard_normal((B, S, E)) * amp),
            "w_out": bf(np.random.standard_normal((H, D, E)) * 1.5 / np.sqrt(HD) / s.reshape(H, D, 1)),
            "scale2": bf(np.random.standard_normal(E) * t),
            "w_gate": bf(np.random.standard_normal((E, F)) / np.sqrt(E) / t[:, None]),
            "w_up": bf(np.random.standard_normal((E, F)) / np.sqrt(E) / t[:, None])}


def reference(attn, x, w_out, scale2, w_gate, w_up):
    a = f64(attn).reshape(B * S, HD)
    h = f64(x).reshape(B * S, E) + (mxq(a, 1, "e4m3") @ mxq(f64(w_out).reshape(HD, E), 0, "e4m3"))
    hq = mxq(rmsnorm(h, f64(scale2)), 1, "e4m3")
    act = gelu_tanh(hq @ mxq(f64(w_gate), 0, "e4m3")) * (hq @ mxq(f64(w_up), 0, "e4m3"))
    return h.reshape(B, S, E), act.reshape(B, S, F)

@@ -1,0 +1,273 @@
+from contextlib import ExitStack
+
+import concourse.mybir as mybir
+from concourse.masks import make_identity
+
+F32 = mybir.dt.float32
+BF16 = mybir.dt.bfloat16
+U32 = mybir.dt.uint32
+U8 = mybir.dt.uint8
+FP8X4 = mybir.dt.float8_e4m3fn_x4
+ACT = mybir.ActivationFunctionType
+ALU = mybir.AluOpType
+
+P = 128
+PACK = 4
+K_PASS = P * PACK
+TOKENS = 512
+E = 1024
+F = 4096
+M_TILES = TOKENS // P
+PASSES = E // K_PASS
+N_TILE = 512
+LOAD_COLS = 1024
+EPS = 1e-6
+CHUNKS = F // N_TILE
+UNITS = CHUNKS * PASSES
+PAIRS = CHUNKS * M_TILES // 2
+LOADS = 2 * PASSES * (F // LOAD_COLS)
+RAW_BUFS = 8
+BANK_TAGS = ("gate", "up")
+
+FLOPS = 2 * TOKENS * E * (E + 2 * F)
+
+
+def regroup(copy, grouped, rows):
+    copy(
+        out=grouped.rearrange("p (c i) t -> p c t i", i=4),
+        in_=rows.rearrange("p t (c i) -> p c t i", i=4),
+    )
+
+
+def tile_block_pb_kernel(tc, attn, x, w_out, scale2, w_gate, w_up, out_0, out_1):
+    nc = tc.nc
+    attn_rows = attn.rearrange("b s i d -> (b s) (i d)")
+    x_rows = x.rearrange("b s e -> (b s) e")
+    w_out_rows = w_out.rearrange("i d e -> (i d) e")
+    h_rows = out_0.rearrange("b s e -> (b s) e")
+    act_rows = out_1.rearrange("b s f -> (b s) f")
+    gate_rows = w_gate.rearrange("(g p t) n -> g p t n", t=PACK, p=P)
+    up_rows = w_up.rearrange("(g p t) n -> g p t n", t=PACK, p=P)
+    out_rows = w_out_rows.rearrange("(g p t) n -> g p t n", t=PACK, p=P)
+
+    with ExitStack() as ctx:
+        const = ctx.enter_context(tc.tile_pool(name="const", bufs=1))
+        keep = ctx.enter_context(tc.tile_pool(name="keep", bufs=1))
+        raw_pool = ctx.enter_context(tc.tile_pool(name="raw", bufs=RAW_BUFS))
+        stage = ctx.enter_context(tc.tile_pool(name="stage", bufs=3))
+        code_pool = ctx.enter_context(tc.tile_pool(name="codes", bufs=3))
+        work = ctx.enter_context(tc.tile_pool(name="work", bufs=4))
+        psum = ctx.enter_context(tc.psum_pool(name="psum", bufs=4))
+        ctx.enter_context(tc.manual_schedule())
+
+        raw_of = {}
+        grouped_of = {}
+        codes_of = {}
+        banks_of = {}
+        gated_of = {}
+
+        def load_weights(k):
+            q, rest = divmod(k, 2 * PASSES)
+            g, w = divmod(rest, 2)
+            rows = (gate_rows, up_rows)[w]
+            raw = raw_pool.tile([P, PACK, LOAD_COLS], BF16, tag="raw", name="raw_w")
+            nc.sync.dma_start(out=raw[:], in_=rows[g][:, :, q * LOAD_COLS : (q + 1) * LOAD_COLS])
+            raw_of[(w, g, q)] = raw
+
+        def regroup_unit(i):
+            j, g = divmod(i, PASSES)
+            q, c = divmod(j, LOAD_COLS // N_TILE)
+            cols = slice(c * N_TILE, (c + 1) * N_TILE)
+            grouped = stage.tile([P, 2, N_TILE, PACK], BF16, align_bytes=64, tag="grouped", name="grouped")
+            regroup(nc.vector.tensor_copy, grouped[:, 0], raw_of[(0, g, q)][:, :, cols])
+            regroup(nc.scalar.copy, grouped[:, 1], raw_of[(1, g, q)][:, :, cols])
+            grouped_of[i] = grouped
+
+        def quantise_unit(i):
+            j, g = divmod(i, PASSES)
+            if g == 0:
+                w_codes = code_pool.tile([P, PASSES, 2, N_TILE], U32, align_bytes=64, tag="w_codes", name="w_codes")
+                w_scales = code_pool.tile([P, PASSES, 2, N_TILE], U8, align_bytes=64, tag="w_scales", name="w_scales")
+                codes_of[j] = (w_codes, w_scales)
+            w_codes, w_scales = codes_of[j]
+            nc.vector.quantize_mx(
+                out=w_codes[:, g].rearrange("p w n -> p (w n)").bitcast(FP8X4),
+                scales=w_scales[:, g].rearrange("p w n -> p (w n)"),
+                in_=grouped_of[i][:].rearrange("p w n t -> p (w n t)"),
+            )
+
+        ident_f32 = const.tile([P, P], F32)
+        make_identity(nc, ident_f32[:])
+        ones = const.tile([P, P], BF16)
+        nc.vector.memset(ones[:], 1.0)
+        eps = const.tile([P, 1], F32)
+        nc.vector.memset(eps[:], EPS)
+        gain_row = const.tile([P, E], BF16)
+        nc.vector.memset(gain_row[:], 0.0)
+        warm = const.tile([P, 1], F32)
+        nc.scalar.activation(out=warm[:], in_=eps[:], func=ACT.Sqrt)
+
+        w_out_raw = []
+        for g in range(PASSES):
+            raw = raw_pool.tile([P, PACK, LOAD_COLS], BF16, tag="raw", name="raw_o")
+            nc.sync.dma_start(out=raw[:], in_=out_rows[g])
+            w_out_raw.append(raw)
+        a_sb = keep.tile([P, M_TILES, E], BF16)
+        for m in range(M_TILES):
+            nc.sync.dma_start(out=a_sb[:, m, :], in_=attn_rows[m * P : (m + 1) * P, :])
+        nc.sync.dma_start(out=gain_row[0:1, :], in_=scale2.unsqueeze(0))
+        x_sb = keep.tile([P, M_TILES, E], BF16)
+        for m in range(M_TILES):
+            nc.sync.dma_start(out=x_sb[:, m, :], in_=x_rows[m * P : (m + 1) * P, :])
+        for k in range(RAW_BUFS - PASSES):
+            load_weights(k)
+
+        wo_codes = keep.tile([P, PASSES, E], U32, align_bytes=64)
+        wo_scales = keep.tile([P, PASSES, E], U8, align_bytes=64)
+        for g in range(PASSES):
+            grouped = stage.tile([P, 2, N_TILE, PACK], BF16, align_bytes=64, tag="grouped", name="grouped")
+            regroup(nc.vector.tensor_copy, grouped[:, 0], w_out_raw[g][:, :, 0:N_TILE])
+            regroup(nc.scalar.copy, grouped[:, 1], w_out_raw[g][:, :, N_TILE : 2 * N_TILE])
+            nc.vector.quantize_mx(
+                out=wo_codes[:, g, :].bitcast(FP8X4),
+                scales=wo_scales[:, g, :],
+                in_=grouped[:].rearrange("p w n t -> p (w n t)"),
+            )
+        for k in range(RAW_BUFS - PASSES, RAW_BUFS):
+            load_weights(k)
+
+        def transpose_words(words, words_t):
+            for g in range(PASSES):
+                for u in range(2):
+                    w0 = 2 * g * P
+                    nc.tensor.transpose(words_t[:, g, u, :], words[:, w0 + u : w0 + 2 * P : 2], ident_f32[:])
+
+        a_grouped = keep.tile([P, M_TILES, PASSES * P * PACK], BF16, align_bytes=64)
+        a_codes = keep.tile([P, M_TILES, PASSES, P], U32, align_bytes=64)
+        a_scales = keep.tile([P, M_TILES, PASSES, P], U8, align_bytes=64)
+        for m in range(M_TILES):
+            a_words = a_sb[:, m, :].bitcast(F32)
+            a_t = psum.tile([P, PASSES, 2, P], F32, tag=BANK_TAGS[m % 2], name="a_t")
+            transpose_words(a_words, a_t)
+            nc.scalar.copy(
+                out=a_grouped[:, m, :].bitcast(F32).rearrange("p (g r u) -> p g r u", g=PASSES, u=2),
+                in_=a_t[:].rearrange("p g u r -> p g r u"),
+            )
+        for m in range(M_TILES):
+            nc.vector.quantize_mx(
+                out=a_codes[:, m].rearrange("p g r -> p (g r)").bitcast(FP8X4),
+                scales=a_scales[:, m].rearrange("p g r -> p (g r)"),
+                in_=a_grouped[:, m, :],
+            )
+
+        gain = const.tile([P, E], F32)
+        for n in range(E // N_TILE):
+            cols = slice(n * N_TILE, (n + 1) * N_TILE)
+            spread = psum.tile([P, N_TILE], F32, tag=BANK_TAGS[n], name="spread")
+            nc.tensor.matmul(out=spread[:], lhsT=ones[:], rhs=gain_row[:, cols], start=True, stop=True)
+            nc.scalar.copy(out=gain[:, cols], in_=spread[:])
+
+        h_sb = keep.tile([P, M_TILES, E], F32)
+        sumsq = keep.tile([P, M_TILES], F32)
+        for m in range(M_TILES):
+            for n in range(E // N_TILE):
+                cols = slice(n * N_TILE, (n + 1) * N_TILE)
+                acc = psum.tile([P, N_TILE], F32, tag=BANK_TAGS[n], name="acc")
+                for g in range(PASSES):
+                    nc.tensor.matmul_mx(
+                        out=acc[:],
+                        lhsT=a_codes[:, m, g, :].bitcast(FP8X4),
+                        lhsT_scale=a_scales[:, m, g, :],
+                        rhs=wo_codes[:, g, cols].bitcast(FP8X4),
+                        rhs_scale=wo_scales[:, g, cols],
+                        start=(g == 0),
+                        stop=(g == PASSES - 1),
+                    )
+                nc.vector.tensor_tensor(out=h_sb[:, m, cols], in0=acc[:], in1=x_sb[:, m, cols], op=ALU.add)
+            nc.sync.dma_start(out=h_rows[m * P : (m + 1) * P, :], in_=h_sb[:, m, :])
+            squares = work.tile([P, E], BF16, tag="squares", name="squares")
+            nc.scalar.activation(out=squares[:], in_=h_sb[:, m, :], func=ACT.Square, accum_out=sumsq[:, m : m + 1])
+
+        std = keep.tile([P, M_TILES], F32)
+        nc.scalar.activation(out=std[:], in_=sumsq[:], func=ACT.Sqrt, scale=1.0 / E, bias=eps[:, 0:1])
+        regroup_unit(0)
+        rstd = keep.tile([P, M_TILES], F32)
+        nc.vector.reciprocal(out=rstd[:], in_=std[:])
+
+        h_grouped = keep.tile([P, M_TILES, PASSES, P, PACK], BF16, align_bytes=64)
+        hn_codes = keep.tile([P, M_TILES, PASSES, P], U32, align_bytes=64)
+        hn_scales = keep.tile([P, M_TILES, PASSES, P], U8, align_bytes=64)
+        for m in range(M_TILES):
+            hn = work.tile([P, E], BF16, tag="hn", name="hn")
+            nc.vector.scalar_tensor_tensor(
+                out=hn[:], in0=h_sb[:, m, :], scalar=rstd[:, m : m + 1], in1=gain[:], op0=ALU.mult, op1=ALU.mult
+            )
+            hn_t = psum.tile([P, PASSES, 2, P], F32, tag=BANK_TAGS[m % 2], name="hn_t")
+            transpose_words(hn[:].bitcast(F32), hn_t)
+            nc.scalar.copy(
+                out=h_grouped[:, m].rearrange("p g r t -> p (g r t)").bitcast(F32).rearrange(
+                    "p (g r u) -> p g r u", g=PASSES, u=2
+                ),
+                in_=hn_t[:].rearrange("p g u r -> p g r u"),
+            )
+        regroup_unit(1)
+        quantise_unit(0)
+        for m in range(M_TILES):
+            nc.vector.quantize_mx(
+                out=hn_codes[:, m].rearrange("p g r -> p (g r)").bitcast(FP8X4),
+                scales=hn_scales[:, m].rearrange("p g r -> p (g r)"),
+                in_=h_grouped[:, m].rearrange("p g r t -> p (g r t)"),
+            )
+
+        def token_tiles(r):
+            j, half = divmod(r, 2)
+            return [(j, 2 * half), (j, 2 * half + 1)]
+
+        def multiply_pair(r):
+            for j, m in token_tiles(r):
+                acc_gate = psum.tile([P, N_TILE], F32, tag="gate", name="acc_gate")
+                acc_up = psum.tile([P, N_TILE], F32, tag="up", name="acc_up")
+                banks_of[(j, m)] = (acc_gate, acc_up)
+            for w in range(2):
+                for j, m in token_tiles(r):
+                    w_codes, w_scales = codes_of[j]
+                    for g in range(PASSES):
+                        nc.tensor.matmul_mx(
+                            out=banks_of[(j, m)][w][:],
+                            lhsT=hn_codes[:, m, g, :].bitcast(FP8X4),
+                            lhsT_scale=hn_scales[:, m, g, :],
+                            rhs=w_codes[:, g, w, :].bitcast(FP8X4),
+                            rhs_scale=w_scales[:, g, w, :],
+                            start=(g == 0),
+                            stop=(g == PASSES - 1),
+                        )
+
+        def gelu_pair(r):
+            gated = work.tile([P, 2, N_TILE], F32, tag="gated", name="gated")
+            for half, (j, m) in enumerate(token_tiles(r)):
+                nc.scalar.activation(out=gated[:, half, :], in_=banks_of[(j, m)][0][:], func=ACT.Gelu_apprx_tanh)
+            gated_of[r] = gated
+
+        def product_pair(r):
+            gated = gated_of[r]
+            for half, (j, m) in reversed(list(enumerate(token_tiles(r)))):
+                nc.vector.tensor_tensor(
+                    out=gated[:, half, :], in0=banks_of[(j, m)][1][:], in1=gated[:, half, :], op=ALU.mult
+                )
+                nc.sync.dma_start(
+                    out=act_rows[m * P : (m + 1) * P, j * N_TILE : (j + 1) * N_TILE], in_=gated[:, half, :]
+                )
+
+        for i in range(2, UNITS + 4):
+            if i < UNITS:
+                regroup_unit(i)
+            if i <= UNITS:
+                quantise_unit(i - 1)
+            if i + RAW_BUFS - 2 < LOADS:
+                load_weights(i + RAW_BUFS - 2)
+            if 0 <= i - 4:
+                product_pair(i - 4)
+            if i - 2 < PAIRS:
+                multiply_pair(i - 2)
+            if 0 <= i - 3 < PAIRS:
+                gelu_pair(i - 3)

@@ -10,6 +10,7 @@ U8 = mybir.dt.uint8
 FP8X4 = mybir.dt.float8_e4m3fn_x4
 ACT = mybir.ActivationFunctionType
 ALU = mybir.AluOpType
+WIDTHS = (512, 512, 512, 512, 512, 512, 512, 256, 256)
 
 P = 128
 PACK = 4
@@ -22,12 +23,9 @@ PASSES = E // K_PASS
 N_TILE = 512
 LOAD_COLS = 1024
 EPS = 1e-6
-CHUNKS = F // N_TILE
-UNITS = CHUNKS * PASSES
-PAIRS = CHUNKS * M_TILES // 2
 LOADS = 2 * PASSES * (F // LOAD_COLS)
 RAW_BUFS = 8
-BANK_TAGS = ("gate", "up")
+TURN_COLS = 256
 
 FLOPS = 2 * TOKENS * E * (E + 2 * F)
 
@@ -43,12 +41,11 @@ def tile_block_pb_kernel(tc, attn, x, w_out, scale2, w_gate, w_up, out_0, out_1)
     nc = tc.nc
     attn_rows = attn.rearrange("b s i d -> (b s) (i d)")
     x_rows = x.rearrange("b s e -> (b s) e")
-    w_out_rows = w_out.rearrange("i d e -> (i d) e")
     h_rows = out_0.rearrange("b s e -> (b s) e")
-    act_rows = out_1.rearrange("b s f -> (b s) f")
-    gate_rows = w_gate.rearrange("(g p t) n -> g p t n", t=PACK, p=P)
-    up_rows = w_up.rearrange("(g p t) n -> g p t n", t=PACK, p=P)
-    out_rows = w_out_rows.rearrange("(g p t) n -> g p t n", t=PACK, p=P)
+    act_rows = out_1.rearrange("b s f -> (b s) f").rearrange("(m p) f -> p m f", p=P)
+    out_w = w_out.rearrange("i d e -> (i d) e").rearrange("(g p t) n -> g p t n", t=PACK, p=P)
+    gate_w = w_gate.rearrange("(g p t) n -> g p t n", t=PACK, p=P)
+    up_w = w_up.rearrange("(g p t) n -> g p t n", t=PACK, p=P)
 
     with ExitStack() as ctx:
         const = ctx.enter_context(tc.tile_pool(name="const", bufs=1))
@@ -57,7 +54,7 @@ def tile_block_pb_kernel(tc, attn, x, w_out, scale2, w_gate, w_up, out_0, out_1)
         stage = ctx.enter_context(tc.tile_pool(name="stage", bufs=3))
         code_pool = ctx.enter_context(tc.tile_pool(name="codes", bufs=3))
         work = ctx.enter_context(tc.tile_pool(name="work", bufs=4))
-        psum = ctx.enter_context(tc.psum_pool(name="psum", bufs=4))
+        psum = ctx.enter_context(tc.psum_pool(name="psum", bufs=3 if 0 or 0 else 4))
         ctx.enter_context(tc.manual_schedule())
 
         raw_of = {}
@@ -65,76 +62,129 @@ def tile_block_pb_kernel(tc, attn, x, w_out, scale2, w_gate, w_up, out_0, out_1)
         codes_of = {}
         banks_of = {}
         gated_of = {}
+        turned_of = {}
 
         def load_weights(k):
             q, rest = divmod(k, 2 * PASSES)
             g, w = divmod(rest, 2)
-            rows = (gate_rows, up_rows)[w]
             raw = raw_pool.tile([P, PACK, LOAD_COLS], BF16, tag="raw", name="raw_w")
-            nc.sync.dma_start(out=raw[:], in_=rows[g][:, :, q * LOAD_COLS : (q + 1) * LOAD_COLS])
+            nc.sync.dma_start(out=raw[:], in_=(gate_w, up_w)[w][g][:, :, q * LOAD_COLS : (q + 1) * LOAD_COLS])
             raw_of[(w, g, q)] = raw
 
-        def regroup_unit(i):
-            j, g = divmod(i, PASSES)
-            q, c = divmod(j, LOAD_COLS // N_TILE)
-            cols = slice(c * N_TILE, (c + 1) * N_TILE)
-            grouped = stage.tile([P, 2, N_TILE, PACK], BF16, align_bytes=64, tag="grouped", name="grouped")
-            regroup(nc.vector.tensor_copy, grouped[:, 0], raw_of[(0, g, q)][:, :, cols])
-            regroup(nc.scalar.copy, grouped[:, 1], raw_of[(1, g, q)][:, :, cols])
-            grouped_of[i] = grouped
+        chunks = []
+        col0 = 0
+        for width in WIDTHS:
+            chunks.append((col0, width))
+            col0 += width
+        units = [(c, g) for c in range(len(chunks)) for g in range(PASSES)]
 
-        def quantise_unit(i):
-            j, g = divmod(i, PASSES)
+        def unit_rows(u, w):
+            c, g = units[u]
+            col0, width = chunks[c]
+            q, n0 = divmod(col0, LOAD_COLS)
+            return raw_of[(w, g, q)][:, :, n0 : n0 + width]
+
+        def tshare(u):
+            return min(0, chunks[units[u][0]][1]) if u < 99 else 0
+
+        def vshare(u):
+            width = chunks[units[u][0]][1]
+            return 512 * width // 512 if u > 1 else width
+
+        def turn(rows, n0):
+            bank = psum.tile([P, TURN_COLS, PACK], BF16, tag="turn", name="bank", bufs=2)
+            for first in range(0, TURN_COLS, P):
+                nc.tensor.matmul(
+                    out=bank[:, first : first + P, :],
+                    lhsT=ident_bf16[:],
+                    rhs=rows[:, :, n0 + first : n0 + first + P].rearrange("p t n -> p n t"),
+                    start=True,
+                    stop=True,
+                )
+            return bank
+
+        def turn_unit(u):
+            turned_of[u] = [(n0, turn(unit_rows(u, 1), n0)) for n0 in range(0, tshare(u), TURN_COLS)]
+
+        def open_unit(u):
+            width = chunks[units[u][0]][1]
+            grouped_of[u] = stage.tile([P, 2, width, PACK], BF16, align_bytes=64, tag="grouped", name="grouped")
+
+        def regroup_vector(u):
+            if u not in grouped_of: open_unit(u)
+            a = vshare(u)
+            regroup(nc.vector.tensor_copy, grouped_of[u][:, 0, 0:a], unit_rows(u, 0)[:, :, 0:a])
+
+        def copy_turned(u):
+            for n0, bank in turned_of.get(u, []):
+                nc.scalar.copy(out=grouped_of[u][:, 1, n0 : n0 + TURN_COLS, :], in_=bank[:])
+
+        def regroup_scalar(u, part=-1):
+            width = chunks[units[u][0]][1]
+            a, lo = vshare(u), tshare(u)
+            if part >= 0:
+                n0 = part * 256
+                regroup(nc.scalar.copy, grouped_of[u][:, 1, n0:n0 + 256], unit_rows(u, 1)[:, :, n0:n0 + 256])
+                return
+            if width > lo:
+                regroup(nc.scalar.copy, grouped_of[u][:, 1, lo:width], unit_rows(u, 1)[:, :, lo:width])
+            if a < width:
+                regroup(nc.scalar.copy, grouped_of[u][:, 0, a:], unit_rows(u, 0)[:, :, a:])
+
+        def quantise_unit(u):
+            c, g = units[u]
+            width = chunks[c][1]
             if g == 0:
-                w_codes = code_pool.tile([P, PASSES, 2, N_TILE], U32, align_bytes=64, tag="w_codes", name="w_codes")
-                w_scales = code_pool.tile([P, PASSES, 2, N_TILE], U8, align_bytes=64, tag="w_scales", name="w_scales")
-                codes_of[j] = (w_codes, w_scales)
-            w_codes, w_scales = codes_of[j]
+                w_codes = code_pool.tile([P, PASSES, 2, width], U32, align_bytes=64, tag="w_codes", name="w_codes")
+                w_scales = code_pool.tile([P, PASSES, 2, width], U8, align_bytes=64, tag="w_scales", name="w_scales")
+                codes_of[c] = (w_codes, w_scales)
+            w_codes, w_scales = codes_of[c]
             nc.vector.quantize_mx(
                 out=w_codes[:, g].rearrange("p w n -> p (w n)").bitcast(FP8X4),
                 scales=w_scales[:, g].rearrange("p w n -> p (w n)"),
-                in_=grouped_of[i][:].rearrange("p w n t -> p (w n t)"),
+                in_=grouped_of[u][:].rearrange("p w n t -> p (w n t)"),
             )
 
+        ident_bf16 = const.tile([P, P], BF16)
+        if 0 or 0: make_identity(nc, ident_bf16[:])
         ident_f32 = const.tile([P, P], F32)
         make_identity(nc, ident_f32[:])
+        gain_row = const.tile([P, E], BF16)
+        nc.vector.memset(gain_row[:], 0.0)
         ones = const.tile([P, P], BF16)
         nc.vector.memset(ones[:], 1.0)
         eps = const.tile([P, 1], F32)
         nc.vector.memset(eps[:], EPS)
-        gain_row = const.tile([P, E], BF16)
-        nc.vector.memset(gain_row[:], 0.0)
         warm = const.tile([P, 1], F32)
         nc.scalar.activation(out=warm[:], in_=eps[:], func=ACT.Sqrt)
 
-        w_out_raw = []
-        for g in range(PASSES):
-            raw = raw_pool.tile([P, PACK, LOAD_COLS], BF16, tag="raw", name="raw_o")
-            nc.sync.dma_start(out=raw[:], in_=out_rows[g])
-            w_out_raw.append(raw)
+        H = E // 2
         a_sb = keep.tile([P, M_TILES, E], BF16)
-        for m in range(M_TILES):
-            nc.sync.dma_start(out=a_sb[:, m, :], in_=attn_rows[m * P : (m + 1) * P, :])
-        nc.sync.dma_start(out=gain_row[0:1, :], in_=scale2.unsqueeze(0))
         x_sb = keep.tile([P, M_TILES, E], BF16)
-        for m in range(M_TILES):
-            nc.sync.dma_start(out=x_sb[:, m, :], in_=x_rows[m * P : (m + 1) * P, :])
-        for k in range(RAW_BUFS - PASSES):
-            load_weights(k)
+        nc.sync.dma_start(out=gain_row[0:1, :], in_=scale2.unsqueeze(0))
+        wo_raw = {}
+
+        def load_out(n, g):
+            if n != 1:
+                wo_raw[g] = raw_pool.tile([P, PACK, LOAD_COLS], BF16, tag="raw", name="raw_o")
+            cols = (slice(0, H), slice(H, E), slice(0, E))[n]
+            nc.sync.dma_start(out=wo_raw[g][:, :, cols], in_=out_w[g][:, :, cols])
+
+        def load_attn(m): nc.sync.dma_start(out=a_sb[:, m, :], in_=attn_rows[m * P : (m + 1) * P, :])
+        def load_x(m): nc.sync.dma_start(out=x_sb[:, m, :], in_=x_rows[m * P : (m + 1) * P, :])
+        gain = const.tile([P, E], F32)
+        def spread_gain():
+            for n in range(E // N_TILE):
+                cols = slice(n * N_TILE, (n + 1) * N_TILE)
+                spread = psum.tile([P, N_TILE], F32, tag=("gate", "up")[n], name="spread")
+                nc.tensor.matmul(out=spread[:], lhsT=ones[:], rhs=gain_row[:, cols], start=True, stop=True)
+                nc.scalar.copy(out=gain[:, cols], in_=spread[:])
 
         wo_codes = keep.tile([P, PASSES, E], U32, align_bytes=64)
         wo_scales = keep.tile([P, PASSES, E], U8, align_bytes=64)
-        for g in range(PASSES):
-            grouped = stage.tile([P, 2, N_TILE, PACK], BF16, align_bytes=64, tag="grouped", name="grouped")
-            regroup(nc.vector.tensor_copy, grouped[:, 0], w_out_raw[g][:, :, 0:N_TILE])
-            regroup(nc.scalar.copy, grouped[:, 1], w_out_raw[g][:, :, N_TILE : 2 * N_TILE])
-            nc.vector.quantize_mx(
-                out=wo_codes[:, g, :].bitcast(FP8X4),
-                scales=wo_scales[:, g, :],
-                in_=grouped[:].rearrange("p w n t -> p (w n t)"),
-            )
-        for k in range(RAW_BUFS - PASSES, RAW_BUFS):
-            load_weights(k)
+        a_grouped = keep.tile([P, M_TILES, PASSES * P * PACK], BF16, align_bytes=64)
+        a_codes = keep.tile([P, M_TILES, PASSES, P], U32, align_bytes=64)
+        a_scales = keep.tile([P, M_TILES, PASSES, P], U8, align_bytes=64)
 
         def transpose_words(words, words_t):
             for g in range(PASSES):
@@ -142,132 +192,248 @@ def tile_block_pb_kernel(tc, attn, x, w_out, scale2, w_gate, w_up, out_0, out_1)
                     w0 = 2 * g * P
                     nc.tensor.transpose(words_t[:, g, u, :], words[:, w0 + u : w0 + 2 * P : 2], ident_f32[:])
 
-        a_grouped = keep.tile([P, M_TILES, PASSES * P * PACK], BF16, align_bytes=64)
-        a_codes = keep.tile([P, M_TILES, PASSES, P], U32, align_bytes=64)
-        a_scales = keep.tile([P, M_TILES, PASSES, P], U8, align_bytes=64)
-        for m in range(M_TILES):
-            a_words = a_sb[:, m, :].bitcast(F32)
-            a_t = psum.tile([P, PASSES, 2, P], F32, tag=BANK_TAGS[m % 2], name="a_t")
-            transpose_words(a_words, a_t)
+        def words_out(grouped, words_t):
             nc.scalar.copy(
-                out=a_grouped[:, m, :].bitcast(F32).rearrange("p (g r u) -> p g r u", g=PASSES, u=2),
-                in_=a_t[:].rearrange("p g u r -> p g r u"),
+                out=grouped.bitcast(F32).rearrange("p (g r u) -> p g r u", g=PASSES, u=2),
+                in_=words_t[:].rearrange("p g u r -> p g r u"),
             )
-        for m in range(M_TILES):
+
+        wo_grouped = {}
+        def regroup_out(n, g):
+            if n != 1:
+                wo_grouped[g] = stage.tile([P, E, PACK], BF16, align_bytes=64, tag="grouped", name="grouped")
+            first, last = ((0, H), (H, E), (0, E))[n]
+            cut = first + (320, 320, 640)[n]
+            rows = wo_raw[g]
+            regroup(nc.vector.tensor_copy, wo_grouped[g][:, first:cut], rows[:, :, first:cut])
+            if 0:
+                for n0 in range(cut, last, TURN_COLS):
+                    nc.scalar.copy(out=wo_grouped[g][:, n0 : n0 + TURN_COLS], in_=turn(rows, n0)[:])
+            elif cut < last:
+                regroup(nc.scalar.copy, wo_grouped[g][:, cut:last], rows[:, :, cut:last])
+
+        def quantise_out(g):
+            nc.vector.quantize_mx(
+                out=wo_codes[:, g].bitcast(FP8X4),
+                scales=wo_scales[:, g],
+                in_=wo_grouped[g][:].rearrange("p n t -> p (n t)"),
+            )
+
+        def turn_attn(m):
+            a_t = psum.tile([P, PASSES, 2, P], F32, tag=("gate", "up")[m % 2], name="a_t")
+            transpose_words(a_sb[:, m, :].bitcast(F32), a_t)
+            words_out(a_grouped[:, m, :], a_t)
+
+        def quantise_attn(m):
             nc.vector.quantize_mx(
                 out=a_codes[:, m].rearrange("p g r -> p (g r)").bitcast(FP8X4),
                 scales=a_scales[:, m].rearrange("p g r -> p (g r)"),
                 in_=a_grouped[:, m, :],
             )
 
-        gain = const.tile([P, E], F32)
-        for n in range(E // N_TILE):
-            cols = slice(n * N_TILE, (n + 1) * N_TILE)
-            spread = psum.tile([P, N_TILE], F32, tag=BANK_TAGS[n], name="spread")
-            nc.tensor.matmul(out=spread[:], lhsT=ones[:], rhs=gain_row[:, cols], start=True, stop=True)
-            nc.scalar.copy(out=gain[:, cols], in_=spread[:])
-
         h_sb = keep.tile([P, M_TILES, E], F32)
-        sumsq = keep.tile([P, M_TILES], F32)
-        for m in range(M_TILES):
-            for n in range(E // N_TILE):
-                cols = slice(n * N_TILE, (n + 1) * N_TILE)
-                acc = psum.tile([P, N_TILE], F32, tag=BANK_TAGS[n], name="acc")
-                for g in range(PASSES):
-                    nc.tensor.matmul_mx(
-                        out=acc[:],
-                        lhsT=a_codes[:, m, g, :].bitcast(FP8X4),
-                        lhsT_scale=a_scales[:, m, g, :],
-                        rhs=wo_codes[:, g, cols].bitcast(FP8X4),
-                        rhs_scale=wo_scales[:, g, cols],
-                        start=(g == 0),
-                        stop=(g == PASSES - 1),
-                    )
-                nc.vector.tensor_tensor(out=h_sb[:, m, cols], in0=acc[:], in1=x_sb[:, m, cols], op=ALU.add)
-            nc.sync.dma_start(out=h_rows[m * P : (m + 1) * P, :], in_=h_sb[:, m, :])
-            squares = work.tile([P, E], BF16, tag="squares", name="squares")
-            nc.scalar.activation(out=squares[:], in_=h_sb[:, m, :], func=ACT.Square, accum_out=sumsq[:, m : m + 1])
-
-        std = keep.tile([P, M_TILES], F32)
-        nc.scalar.activation(out=std[:], in_=sumsq[:], func=ACT.Sqrt, scale=1.0 / E, bias=eps[:, 0:1])
-        regroup_unit(0)
-        rstd = keep.tile([P, M_TILES], F32)
-        nc.vector.reciprocal(out=rstd[:], in_=std[:])
-
-        h_grouped = keep.tile([P, M_TILES, PASSES, P, PACK], BF16, align_bytes=64)
+        sumsq = keep.tile([P, M_TILES, 8], F32)
+        std = keep.tile([P, M_TILES, 8], F32)
+        rstd = keep.tile([P, M_TILES, 8], F32)
+        h_grouped = keep.tile([P, M_TILES, PASSES * P * PACK], BF16, align_bytes=64)
         hn_codes = keep.tile([P, M_TILES, PASSES, P], U32, align_bytes=64)
         hn_scales = keep.tile([P, M_TILES, PASSES, P], U8, align_bytes=64)
-        for m in range(M_TILES):
-            hn = work.tile([P, E], BF16, tag="hn", name="hn")
+
+        acc_of = {}
+        hn_of = {}
+        def project(m, n):
+            acc = psum.tile([P, N_TILE], F32, tag=("gate", "up")[m % 2], name="acc")
+            for g in range(PASSES):
+                nc.tensor.matmul_mx(
+                    out=acc[:],
+                    lhsT=a_codes[:, m, g, :].bitcast(FP8X4),
+                    lhsT_scale=a_scales[:, m, g, :],
+                    rhs=wo_codes[:, g, n * H : (n + 1) * H].bitcast(FP8X4),
+                    rhs_scale=wo_scales[:, g, n * H : (n + 1) * H],
+                    start=(g == 0),
+                    stop=(g == PASSES - 1),
+                )
+            acc_of[(m, n)] = acc
+
+        def add(m, n):
+            cols = slice(n * N_TILE, (n + 1) * N_TILE)
+            nc.vector.tensor_tensor(out=h_sb[:, m, cols], in0=acc_of[(m, n)][:], in1=x_sb[:, m, cols], op=ALU.add)
+
+        def square(m):
+            squares = work.tile([P, E], BF16, tag="squares", name="squares", bufs=2)
+            nc.scalar.activation(out=squares[:], in_=h_sb[:, m, :], func=ACT.Square, accum_out=sumsq[:, m, 0:1])
+            nc.scalar.activation(out=std[:, m, 0:1], in_=sumsq[:, m, 0:1], func=ACT.Sqrt, scale=1.0 / E, bias=eps[:, 0:1])
+
+        def store_h(m):
+            nc.sync.dma_start(out=h_rows[m * P : (m + 1) * P, :], in_=h_sb[:, m, :])
+
+        def norm(m):
+            nc.vector.reciprocal(out=rstd[:, m, 0:1], in_=std[:, m, 0:1])
+            hn = work.tile([P, E], BF16, tag="hn", name="hn", bufs=2)
             nc.vector.scalar_tensor_tensor(
-                out=hn[:], in0=h_sb[:, m, :], scalar=rstd[:, m : m + 1], in1=gain[:], op0=ALU.mult, op1=ALU.mult
+                out=hn[:], in0=h_sb[:, m, :], scalar=rstd[:, m, 0:1], in1=gain[:], op0=ALU.mult, op1=ALU.mult
             )
-            hn_t = psum.tile([P, PASSES, 2, P], F32, tag=BANK_TAGS[m % 2], name="hn_t")
-            transpose_words(hn[:].bitcast(F32), hn_t)
-            nc.scalar.copy(
-                out=h_grouped[:, m].rearrange("p g r t -> p (g r t)").bitcast(F32).rearrange(
-                    "p (g r u) -> p g r u", g=PASSES, u=2
-                ),
-                in_=hn_t[:].rearrange("p g u r -> p g r u"),
-            )
-        regroup_unit(1)
-        quantise_unit(0)
-        for m in range(M_TILES):
+            hn_of[m] = hn
+
+        def turn_norm(m):
+            hn_t = psum.tile([P, PASSES, 2, P], F32, tag=("gate", "up")[m % 2], name="hn_t")
+            transpose_words(hn_of[m][:].bitcast(F32), hn_t)
+            words_out(h_grouped[:, m, :], hn_t)
+
+        def quantise_norm(m):
             nc.vector.quantize_mx(
                 out=hn_codes[:, m].rearrange("p g r -> p (g r)").bitcast(FP8X4),
                 scales=hn_scales[:, m].rearrange("p g r -> p (g r)"),
-                in_=h_grouped[:, m].rearrange("p g r t -> p (g r t)"),
+                in_=h_grouped[:, m, :],
             )
 
-        def token_tiles(r):
-            j, half = divmod(r, 2)
-            return [(j, 2 * half), (j, 2 * half + 1)]
+        jobs = []
+        for c, (col0, width) in enumerate(chunks):
+            per = N_TILE // width
+            for m0 in range(0, M_TILES, per):
+                jobs.append((c, m0, per))
 
-        def multiply_pair(r):
-            for j, m in token_tiles(r):
-                acc_gate = psum.tile([P, N_TILE], F32, tag="gate", name="acc_gate")
-                acc_up = psum.tile([P, N_TILE], F32, tag="up", name="acc_up")
-                banks_of[(j, m)] = (acc_gate, acc_up)
+        def multiply(r):
+            c, m0, per = jobs[r]
+            width = chunks[c][1]
+            acc = [psum.tile([P, per, width], F32, tag=tag, name="acc2") for tag in ("gate", "up")]
+            banks_of[r] = acc
+            w_codes, w_scales = codes_of[c]
             for w in range(2):
-                for j, m in token_tiles(r):
-                    w_codes, w_scales = codes_of[j]
+                for k in range(per):
                     for g in range(PASSES):
                         nc.tensor.matmul_mx(
-                            out=banks_of[(j, m)][w][:],
-                            lhsT=hn_codes[:, m, g, :].bitcast(FP8X4),
-                            lhsT_scale=hn_scales[:, m, g, :],
+                            out=acc[w][:, k, :],
+                            lhsT=hn_codes[:, m0 + k, g, :].bitcast(FP8X4),
+                            lhsT_scale=hn_scales[:, m0 + k, g, :],
                             rhs=w_codes[:, g, w, :].bitcast(FP8X4),
                             rhs_scale=w_scales[:, g, w, :],
                             start=(g == 0),
                             stop=(g == PASSES - 1),
                         )
 
-        def gelu_pair(r):
-            gated = work.tile([P, 2, N_TILE], F32, tag="gated", name="gated")
-            for half, (j, m) in enumerate(token_tiles(r)):
-                nc.scalar.activation(out=gated[:, half, :], in_=banks_of[(j, m)][0][:], func=ACT.Gelu_apprx_tanh)
+        def gelu(r):
+            c, m0, per = jobs[r]
+            gated = work.tile([P, per, chunks[c][1]], F32, tag="gated", name="gated", bufs=8)
+            nc.scalar.activation(out=gated[:], in_=banks_of[r][0][:], func=ACT.Gelu_apprx_tanh)
             gated_of[r] = gated
 
-        def product_pair(r):
+        def product(r):
+            c, m0, per = jobs[r]
+            col0, width = chunks[c]
             gated = gated_of[r]
-            for half, (j, m) in reversed(list(enumerate(token_tiles(r)))):
-                nc.vector.tensor_tensor(
-                    out=gated[:, half, :], in0=banks_of[(j, m)][1][:], in1=gated[:, half, :], op=ALU.mult
-                )
-                nc.sync.dma_start(
-                    out=act_rows[m * P : (m + 1) * P, j * N_TILE : (j + 1) * N_TILE], in_=gated[:, half, :]
-                )
+            nc.vector.tensor_tensor(out=gated[:], in0=banks_of[r][1][:], in1=gated[:], op=ALU.mult)
+            nc.sync.dma_start(out=act_rows[:, m0 : m0 + per, col0 : col0 + width], in_=gated[:])
 
-        for i in range(2, UNITS + 4):
-            if i < UNITS:
-                regroup_unit(i)
-            if i <= UNITS:
+        order = [1, 3, 0, 2] + list(range(4, LOADS))
+        loads_done = []
+
+        def load_next():
+            if len(loads_done) < LOADS:
+                load_weights(order[len(loads_done)])
+                loads_done.append(1)
+
+        load_out(0, 0)
+        load_out(1, 0)
+        load_out(2, 1)
+        load_attn(0)
+        load_attn(1)
+        load_attn(2)
+        load_attn(3)
+        load_next()
+        load_x(0)
+        load_x(1)
+        load_x(2)
+        load_x(3)
+        load_next()
+        load_next()
+        load_next()
+        load_next()
+        load_next()
+        spread_gain()
+        regroup_out(0, 0)
+        regroup_out(1, 0)
+        quantise_out(0)
+        regroup_out(2, 1)
+        turn_attn(0)
+        turn_attn(1)
+        turn_attn(2)
+        turn_attn(3)
+        quantise_out(1)
+        quantise_attn(0)
+        quantise_attn(1)
+        quantise_attn(2)
+        quantise_attn(3)
+        project(0, 0)
+        project(0, 1)
+        project(1, 0)
+        project(1, 1)
+        project(2, 0)
+        project(2, 1)
+        open_unit(0)
+        regroup_scalar(0, 0)
+        regroup_scalar(0, 1)
+        project(3, 0)
+        project(3, 1)
+        load_next()
+        load_next()
+        add(0, 0)
+        add(0, 1)
+        square(0)
+        store_h(0)
+        add(1, 0)
+        add(1, 1)
+        square(1)
+        store_h(1)
+        open_unit(1)
+        regroup_scalar(1, 0)
+        norm(0)
+        add(2, 0)
+        add(2, 1)
+        square(2)
+        store_h(2)
+        turn_norm(0)
+        regroup_scalar(1, 1)
+        norm(1)
+        add(3, 0)
+        add(3, 1)
+        square(3)
+        store_h(3)
+        turn_norm(1)
+        norm(2)
+        regroup_vector(0)
+        turn_norm(2)
+        quantise_norm(0)
+        norm(3)
+        turn_norm(3)
+        regroup_vector(1)
+        quantise_unit(0)
+        quantise_norm(1)
+        quantise_norm(2)
+        quantise_norm(3)
+
+        mult = {}
+        for c in range(len(chunks)):
+            mine = [r for r in range(len(jobs)) if jobs[r][0] == c]
+            half = -(-len(mine) // 2)
+            mult[2 * c + 2] = mine[:half]
+            mult[2 * c + 3] = mine[half:]
+        nu = len(units)
+        for i in range(2, nu + 4):
+            if i < nu:
+                regroup_vector(i)
+            if i <= nu:
                 quantise_unit(i - 1)
-            if i + RAW_BUFS - 2 < LOADS:
-                load_weights(i + RAW_BUFS - 2)
-            if 0 <= i - 4:
-                product_pair(i - 4)
-            if i - 2 < PAIRS:
-                multiply_pair(i - 2)
-            if 0 <= i - 3 < PAIRS:
-                gelu_pair(i - 3)
+            load_next()
+            for r in mult.get(i - 2, []):
+                product(r)
+            if i < nu:
+                copy_turned(i)
+            if i < nu:
+                regroup_scalar(i)
+            if i + 1 < nu:
+                turn_unit(i + 1)
+            for r in mult.get(i, []):
+                multiply(r)
+            for r in mult.get(i - 1, []):
+                gelu(r)

@@ -39,10 +39,10 @@ def regroup(copy, grouped, rows):
 
 def tile_block_pb_kernel(tc, attn, x, w_out, scale2, w_gate, w_up, out_0, out_1):
     nc = tc.nc
-    attn_rows = attn.rearrange("b s i d -> (b s) (i d)")
-    x_rows = x.rearrange("b s e -> (b s) e")
-    h_rows = out_0.rearrange("b s e -> (b s) e")
-    act_rows = out_1.rearrange("b s f -> (b s) f").rearrange("(m p) f -> p m f", p=P)
+    attn_rows = attn.rearrange("b s i d -> (b s) (i d)").rearrange("(p m) e -> p m e", p=P)
+    x_rows = x.rearrange("b s e -> (b s) e").rearrange("(p m) e -> p m e", p=P)
+    h_rows = out_0.rearrange("b s e -> (b s) e").rearrange("(p m) e -> p m e", p=P)
+    act_rows = out_1.rearrange("b s f -> (b s) f").rearrange("(p m) f -> p m f", p=P)
     out_w = w_out.rearrange("i d e -> (i d) e").rearrange("(g p t) n -> g p t n", t=PACK, p=P)
     gate_w = w_gate.rearrange("(g p t) n -> g p t n", t=PACK, p=P)
     up_w = w_up.rearrange("(g p t) n -> g p t n", t=PACK, p=P)
@@ -150,7 +150,7 @@ def tile_block_pb_kernel(tc, attn, x, w_out, scale2, w_gate, w_up, out_0, out_1)
         ident_f32 = const.tile([P, P], F32)
         make_identity(nc, ident_f32[:])
         gain_row = const.tile([P, E], BF16)
-        nc.vector.memset(gain_row[:], 0.0)
+        nc.gpsimd.memset(gain_row[:], 0.0)
         ones = const.tile([P, P], BF16)
         nc.vector.memset(ones[:], 1.0)
         eps = const.tile([P, 1], F32)
@@ -161,7 +161,6 @@ def tile_block_pb_kernel(tc, attn, x, w_out, scale2, w_gate, w_up, out_0, out_1)
         H = E // 2
         a_sb = keep.tile([P, M_TILES, E], BF16)
         x_sb = keep.tile([P, M_TILES, E], BF16)
-        nc.sync.dma_start(out=gain_row[0:1, :], in_=scale2.unsqueeze(0))
         wo_raw = {}
 
         def load_out(n, g):
@@ -170,9 +169,13 @@ def tile_block_pb_kernel(tc, attn, x, w_out, scale2, w_gate, w_up, out_0, out_1)
             cols = (slice(0, H), slice(H, E), slice(0, E))[n]
             nc.sync.dma_start(out=wo_raw[g][:, :, cols], in_=out_w[g][:, :, cols])
 
-        def load_attn(m): nc.sync.dma_start(out=a_sb[:, m, :], in_=attn_rows[m * P : (m + 1) * P, :])
-        def load_x(m): nc.sync.dma_start(out=x_sb[:, m, :], in_=x_rows[m * P : (m + 1) * P, :])
+        def load_attn(m): nc.sync.dma_start(out=a_sb[:, m : m + 2, :], in_=attn_rows[:, m : m + 2, :])
+        def load_x(m): nc.sync.dma_start(out=x_sb[:, m : m + 2, :], in_=x_rows[:, m : m + 2, :])
+        def load_gain():
+            nc.sync.dma_start(out=gain_row[0:1, :], in_=scale2.unsqueeze(0))
+
         gain = const.tile([P, E], F32)
+
         def spread_gain():
             for n in range(E // N_TILE):
                 cols = slice(n * N_TILE, (n + 1) * N_TILE)
@@ -235,6 +238,9 @@ def tile_block_pb_kernel(tc, attn, x, w_out, scale2, w_gate, w_up, out_0, out_1)
         sumsq = keep.tile([P, M_TILES, 8], F32)
         std = keep.tile([P, M_TILES, 8], F32)
         rstd = keep.tile([P, M_TILES, 8], F32)
+        sums = keep.tile([P, M_TILES], F32)
+        roots = keep.tile([P, M_TILES], F32)
+        inverse = keep.tile([P, M_TILES], F32)
         h_grouped = keep.tile([P, M_TILES, PASSES * P * PACK], BF16, align_bytes=64)
         hn_codes = keep.tile([P, M_TILES, PASSES, P], U32, align_bytes=64)
         hn_scales = keep.tile([P, M_TILES, PASSES, P], U8, align_bytes=64)
@@ -264,8 +270,25 @@ def tile_block_pb_kernel(tc, attn, x, w_out, scale2, w_gate, w_up, out_0, out_1)
             nc.scalar.activation(out=squares[:], in_=h_sb[:, m, :], func=ACT.Square, accum_out=sumsq[:, m, 0:1])
             nc.scalar.activation(out=std[:, m, 0:1], in_=sumsq[:, m, 0:1], func=ACT.Sqrt, scale=1.0 / E, bias=eps[:, 0:1])
 
+        def square_only(m):
+            squares = work.tile([P, E], BF16, tag="squares", name="squares", bufs=2)
+            nc.scalar.activation(out=squares[:], in_=h_sb[:, m, :], func=ACT.Square, accum_out=sums[:, m : m + 1])
+
+        def root_all():
+            nc.scalar.activation(out=roots[:], in_=sums[:], func=ACT.Sqrt, scale=1.0 / E, bias=eps[:, 0:1])
+
+        def reciprocal_all():
+            nc.vector.reciprocal(out=inverse[:], in_=roots[:])
+
+        def norm_only(m):
+            hn = work.tile([P, E], BF16, tag="hn", name="hn", bufs=2)
+            nc.vector.scalar_tensor_tensor(
+                out=hn[:], in0=h_sb[:, m, :], scalar=inverse[:, m : m + 1], in1=gain[:], op0=ALU.mult, op1=ALU.mult
+            )
+            hn_of[m] = hn
+
         def store_h(m):
-            nc.sync.dma_start(out=h_rows[m * P : (m + 1) * P, :], in_=h_sb[:, m, :])
+            nc.sync.dma_start(out=h_rows[:, m, :], in_=h_sb[:, m, :])
 
         def norm(m):
             nc.vector.reciprocal(out=rstd[:, m, 0:1], in_=std[:, m, 0:1])
@@ -325,7 +348,7 @@ def tile_block_pb_kernel(tc, attn, x, w_out, scale2, w_gate, w_up, out_0, out_1)
             nc.vector.tensor_tensor(out=gated[:], in0=banks_of[r][1][:], in1=gated[:], op=ALU.mult)
             nc.sync.dma_start(out=act_rows[:, m0 : m0 + per, col0 : col0 + width], in_=gated[:])
 
-        order = [1, 3, 0, 2] + list(range(4, LOADS))
+        order = list(range(LOADS))
         loads_done = []
 
         def load_next():
@@ -337,20 +360,15 @@ def tile_block_pb_kernel(tc, attn, x, w_out, scale2, w_gate, w_up, out_0, out_1)
         load_out(1, 0)
         load_out(2, 1)
         load_attn(0)
-        load_attn(1)
         load_attn(2)
-        load_attn(3)
-        load_next()
+        load_gain()
         load_x(0)
-        load_x(1)
         load_x(2)
-        load_x(3)
         load_next()
         load_next()
         load_next()
         load_next()
         load_next()
-        spread_gain()
         regroup_out(0, 0)
         regroup_out(1, 0)
         quantise_out(0)
@@ -364,50 +382,50 @@ def tile_block_pb_kernel(tc, attn, x, w_out, scale2, w_gate, w_up, out_0, out_1)
         quantise_attn(1)
         quantise_attn(2)
         quantise_attn(3)
+        spread_gain()
+        load_next()
+        load_next()
+        load_next()
         project(0, 0)
         project(0, 1)
-        project(1, 0)
-        project(1, 1)
-        project(2, 0)
-        project(2, 1)
-        open_unit(0)
-        regroup_scalar(0, 0)
-        regroup_scalar(0, 1)
-        project(3, 0)
-        project(3, 1)
-        load_next()
-        load_next()
         add(0, 0)
         add(0, 1)
-        square(0)
         store_h(0)
+        square_only(0)
+        project(1, 0)
+        project(1, 1)
         add(1, 0)
         add(1, 1)
-        square(1)
         store_h(1)
-        open_unit(1)
-        regroup_scalar(1, 0)
-        norm(0)
+        square_only(1)
+        project(2, 0)
+        project(2, 1)
         add(2, 0)
         add(2, 1)
-        square(2)
         store_h(2)
-        turn_norm(0)
-        regroup_scalar(1, 1)
-        norm(1)
+        square_only(2)
+        project(3, 0)
+        project(3, 1)
         add(3, 0)
         add(3, 1)
-        square(3)
         store_h(3)
-        turn_norm(1)
-        norm(2)
+        square_only(3)
+        root_all()
         regroup_vector(0)
+        regroup_scalar(0)
+        reciprocal_all()
+        norm_only(0)
+        turn_norm(0)
+        norm_only(1)
+        turn_norm(1)
+        norm_only(2)
         turn_norm(2)
-        quantise_norm(0)
-        norm(3)
+        norm_only(3)
         turn_norm(3)
         regroup_vector(1)
+        regroup_scalar(1)
         quantise_unit(0)
+        quantise_norm(0)
         quantise_norm(1)
         quantise_norm(2)
         quantise_norm(3)

@@ -23,7 +23,7 @@ PASSES = E // K_PASS
 N_TILE = 512
 LOAD_COLS = 1024
 EPS = 1e-6
-LOADS = 2 * PASSES * (F // LOAD_COLS)
+LOADS = 12 if 0 else 2 * PASSES * (F // LOAD_COLS)
 RAW_BUFS = 8
 TURN_COLS = 256
 
@@ -51,7 +51,7 @@ def tile_block_pb_kernel(tc, attn, x, w_out, scale2, w_gate, w_up, out_0, out_1)
         const = ctx.enter_context(tc.tile_pool(name="const", bufs=1))
         keep = ctx.enter_context(tc.tile_pool(name="keep", bufs=1))
         raw_pool = ctx.enter_context(tc.tile_pool(name="raw", bufs=RAW_BUFS))
-        stage = ctx.enter_context(tc.tile_pool(name="stage", bufs=3))
+        stage = ctx.enter_context(tc.tile_pool(name="stage", bufs=2))
         code_pool = ctx.enter_context(tc.tile_pool(name="codes", bufs=3))
         work = ctx.enter_context(tc.tile_pool(name="work", bufs=4))
         psum = ctx.enter_context(tc.psum_pool(name="psum", bufs=3 if 0 or 0 else 4))
@@ -64,7 +64,25 @@ def tile_block_pb_kernel(tc, attn, x, w_out, scale2, w_gate, w_up, out_0, out_1)
         gated_of = {}
         turned_of = {}
 
+        def load_big(k):
+            if k < 8:
+                q, rest = divmod(k, 2 * PASSES)
+                g, w = divmod(rest, 2)
+                if g == 0:
+                    raw_of[(w, q)] = raw_pool.tile([P, PASSES, PACK, LOAD_COLS], BF16, tag="raw", name="raw_w")
+                raw = raw_of[(w, q)][:, g]
+                nc.sync.dma_start(out=raw, in_=(gate_w, up_w)[w][g][:, :, q * LOAD_COLS : (q + 1) * LOAD_COLS])
+                raw_of[(w, g, q)] = raw
+            else:
+                g, w = divmod(k - 8, 2)
+                raw = raw_pool.tile([P, PACK, 2 * LOAD_COLS], BF16, tag="raw", name="raw_b")
+                nc.sync.dma_start(out=raw[:], in_=(gate_w, up_w)[w][g][:, :, 2 * LOAD_COLS : F])
+                for q in (2, 3):
+                    raw_of[(w, g, q)] = raw[:, :, (q - 2) * LOAD_COLS : (q - 1) * LOAD_COLS]
+
         def load_weights(k):
+            if 0:
+                return load_big(k)
             q, rest = divmod(k, 2 * PASSES)
             g, w = divmod(rest, 2)
             raw = raw_pool.tile([P, PACK, LOAD_COLS], BF16, tag="raw", name="raw_w")
@@ -87,9 +105,25 @@ def tile_block_pb_kernel(tc, attn, x, w_out, scale2, w_gate, w_up, out_0, out_1)
         def tshare(u):
             return min(0, chunks[units[u][0]][1]) if u < 99 else 0
 
+        def gshare(u):
+            return 128 * chunks[units[u][0]][1] // 512 if u > 2 else 0
+
         def vshare(u):
             width = chunks[units[u][0]][1]
-            return 512 * width // 512 if u > 1 else width
+            return (512 * width // 512 if u > 1 else width) - (gshare(u) if u % 2 == 0 else 0)
+
+        def regroup_gps(u):
+            open_unit(u)
+            share, width, w = gshare(u), chunks[units[u][0]][1], u % 2
+            if share:
+                nc.gpsimd.tensor_scalar(
+                    out=grouped_of[u][:, w, width - share :, :],
+                    in0=unit_rows(u, w)[:, :, width - share :].rearrange("p t n -> p n t"),
+                    scalar1=1.0,
+                    scalar2=0.0,
+                    op0=ALU.mult,
+                    op1=ALU.add,
+                )
 
         def turn(rows, n0):
             bank = psum.tile([P, TURN_COLS, PACK], BF16, tag="turn", name="bank", bufs=2)
@@ -126,10 +160,12 @@ def tile_block_pb_kernel(tc, attn, x, w_out, scale2, w_gate, w_up, out_0, out_1)
                 n0 = part * 256
                 regroup(nc.scalar.copy, grouped_of[u][:, 1, n0:n0 + 256], unit_rows(u, 1)[:, :, n0:n0 + 256])
                 return
-            if width > lo:
-                regroup(nc.scalar.copy, grouped_of[u][:, 1, lo:width], unit_rows(u, 1)[:, :, lo:width])
-            if a < width:
-                regroup(nc.scalar.copy, grouped_of[u][:, 0, a:], unit_rows(u, 0)[:, :, a:])
+            up_end = width - (gshare(u) if u % 2 else 0)
+            gate_end = width - (0 if u % 2 else gshare(u))
+            if up_end > lo:
+                regroup(nc.scalar.copy, grouped_of[u][:, 1, lo:up_end], unit_rows(u, 1)[:, :, lo:up_end])
+            if a < gate_end:
+                regroup(nc.scalar.copy, grouped_of[u][:, 0, a:gate_end], unit_rows(u, 0)[:, :, a:gate_end])
 
         def quantise_unit(u):
             c, g = units[u]
@@ -159,15 +195,15 @@ def tile_block_pb_kernel(tc, attn, x, w_out, scale2, w_gate, w_up, out_0, out_1)
         nc.scalar.activation(out=warm[:], in_=eps[:], func=ACT.Sqrt)
 
         H = E // 2
-        a_sb = keep.tile([P, M_TILES, E], BF16)
+        a_sb = keep.tile([P, M_TILES, E], BF16, align_bytes=64, tag="tokens")
         x_sb = keep.tile([P, M_TILES, E], BF16)
         wo_raw = {}
 
         def load_out(n, g):
-            if n != 1:
-                wo_raw[g] = raw_pool.tile([P, PACK, LOAD_COLS], BF16, tag="raw", name="raw_o")
-            cols = (slice(0, H), slice(H, E), slice(0, E))[n]
-            nc.sync.dma_start(out=wo_raw[g][:, :, cols], in_=out_w[g][:, :, cols])
+            width = H if n < 2 else E
+            first = H if n == 1 else 0
+            wo_raw[(n, g)] = raw_pool.tile([P, PACK, width], BF16, tag="raw", name="raw_o")
+            nc.sync.dma_start(out=wo_raw[(n, g)][:], in_=out_w[g][:, :, first : first + width])
 
         def load_attn(m): nc.sync.dma_start(out=a_sb[:, m : m + 2, :], in_=attn_rows[:, m : m + 2, :])
         def load_x(m): nc.sync.dma_start(out=x_sb[:, m : m + 2, :], in_=x_rows[:, m : m + 2, :])
@@ -205,15 +241,17 @@ def tile_block_pb_kernel(tc, attn, x, w_out, scale2, w_gate, w_up, out_0, out_1)
         def regroup_out(n, g):
             if n != 1:
                 wo_grouped[g] = stage.tile([P, E, PACK], BF16, align_bytes=64, tag="grouped", name="grouped")
-            first, last = ((0, H), (H, E), (0, E))[n]
-            cut = first + (320, 320, 640)[n]
-            rows = wo_raw[g]
-            regroup(nc.vector.tensor_copy, wo_grouped[g][:, first:cut], rows[:, :, first:cut])
+            width = H if n < 2 else E
+            first = H if n == 1 else 0
+            cut = (320, 320, 640)[n]
+            rows = wo_raw[(n, g)]
+            grouped = wo_grouped[g][:, first : first + width]
+            regroup(nc.vector.tensor_copy, grouped[:, 0:cut], rows[:, :, 0:cut])
             if 0:
-                for n0 in range(cut, last, TURN_COLS):
-                    nc.scalar.copy(out=wo_grouped[g][:, n0 : n0 + TURN_COLS], in_=turn(rows, n0)[:])
-            elif cut < last:
-                regroup(nc.scalar.copy, wo_grouped[g][:, cut:last], rows[:, :, cut:last])
+                for n0 in range(cut, width, TURN_COLS):
+                    nc.scalar.copy(out=grouped[:, n0 : n0 + TURN_COLS], in_=turn(rows, n0)[:])
+            elif cut < width:
+                regroup(nc.scalar.copy, grouped[:, cut:width], rows[:, :, cut:width])
 
         def quantise_out(g):
             nc.vector.quantize_mx(
@@ -241,7 +279,7 @@ def tile_block_pb_kernel(tc, attn, x, w_out, scale2, w_gate, w_up, out_0, out_1)
         sums = keep.tile([P, M_TILES], F32)
         roots = keep.tile([P, M_TILES], F32)
         inverse = keep.tile([P, M_TILES], F32)
-        h_grouped = keep.tile([P, M_TILES, PASSES * P * PACK], BF16, align_bytes=64)
+        h_grouped = keep.tile([P, M_TILES, PASSES * P * PACK], BF16, align_bytes=64, tag="tokens")
         hn_codes = keep.tile([P, M_TILES, PASSES, P], U32, align_bytes=64)
         hn_scales = keep.tile([P, M_TILES, PASSES, P], U8, align_bytes=64)
 
@@ -442,9 +480,11 @@ def tile_block_pb_kernel(tc, attn, x, w_out, scale2, w_gate, w_up, out_0, out_1)
                 regroup_vector(i)
             if i <= nu:
                 quantise_unit(i - 1)
-            load_next()
             for r in mult.get(i - 2, []):
                 product(r)
+            if i + 1 < nu:
+                regroup_gps(i + 1)
+            load_next()
             if i < nu:
                 copy_turned(i)
             if i < nu:

@@ -108,13 +108,17 @@ def tile_block_pb_kernel(tc, attn, x, w_out, scale2, w_gate, w_up, out_0, out_1)
         def gshare(u):
             return 128 * chunks[units[u][0]][1] // 512 if u > 2 else 0
 
+        def gside(u):
+            return (u % 2, 1, 0)[1]
+
         def vshare(u):
             width = chunks[units[u][0]][1]
-            return (512 * width // 512 if u > 1 else width) - (gshare(u) if u % 2 == 0 else 0)
+            return (448 * width // 512 if u > 1 else width) - (gshare(u) if gside(u) == 0 else 0)
 
         def regroup_gps(u):
-            open_unit(u)
-            share, width, w = gshare(u), chunks[units[u][0]][1], u % 2
+            if u not in grouped_of:
+                open_unit(u)
+            share, width, w = gshare(u), chunks[units[u][0]][1], gside(u)
             if share:
                 nc.gpsimd.tensor_scalar(
                     out=grouped_of[u][:, w, width - share :, :],
@@ -144,10 +148,18 @@ def tile_block_pb_kernel(tc, attn, x, w_out, scale2, w_gate, w_up, out_0, out_1)
             width = chunks[units[u][0]][1]
             grouped_of[u] = stage.tile([P, 2, width, PACK], BF16, align_bytes=64, tag="grouped", name="grouped")
 
+        def upshare(u):
+            return 0 * chunks[units[u][0]][1] // 512 if u > 2 else 0
+
         def regroup_vector(u):
-            if u not in grouped_of: open_unit(u)
-            a = vshare(u)
+            if u not in grouped_of:
+                open_unit(u)
+            a, width, b = vshare(u), chunks[units[u][0]][1], upshare(u)
+            if 0 and gshare(u):
+                a += 8
             regroup(nc.vector.tensor_copy, grouped_of[u][:, 0, 0:a], unit_rows(u, 0)[:, :, 0:a])
+            if b:
+                regroup(nc.vector.tensor_copy, grouped_of[u][:, 1, width - b :], unit_rows(u, 1)[:, :, width - b :])
 
         def copy_turned(u):
             for n0, bank in turned_of.get(u, []):
@@ -160,8 +172,8 @@ def tile_block_pb_kernel(tc, attn, x, w_out, scale2, w_gate, w_up, out_0, out_1)
                 n0 = part * 256
                 regroup(nc.scalar.copy, grouped_of[u][:, 1, n0:n0 + 256], unit_rows(u, 1)[:, :, n0:n0 + 256])
                 return
-            up_end = width - (gshare(u) if u % 2 else 0)
-            gate_end = width - (0 if u % 2 else gshare(u))
+            up_end = width - (gshare(u) if gside(u) else 0) - upshare(u)
+            gate_end = width - (0 if gside(u) else gshare(u))
             if up_end > lo:
                 regroup(nc.scalar.copy, grouped_of[u][:, 1, lo:up_end], unit_rows(u, 1)[:, :, lo:up_end])
             if a < gate_end:
@@ -373,18 +385,34 @@ def tile_block_pb_kernel(tc, attn, x, w_out, scale2, w_gate, w_up, out_0, out_1)
                             stop=(g == PASSES - 1),
                         )
 
+        pair_of = {}
+
         def gelu(r):
             c, m0, per = jobs[r]
-            gated = work.tile([P, per, chunks[c][1]], F32, tag="gated", name="gated", bufs=8)
-            nc.scalar.activation(out=gated[:], in_=banks_of[r][0][:], func=ACT.Gelu_apprx_tanh)
+            width = chunks[c][1]
+            if 0 and width == N_TILE and c < 0:
+                if c % 2 == 0:
+                    pair_of[m0] = work.tile([P, 2, N_TILE], F32, tag="gated2", name="gated2", bufs=8 // 2)
+                gated = pair_of[m0][:, c % 2]
+            else:
+                single = work.tile([P, per, width], F32, tag="gated", name="gated", bufs=8 if not 0 else 4)
+                gated = single[:]
+            nc.scalar.activation(out=gated, in_=banks_of[r][0][:] if per > 1 else banks_of[r][0][:, 0, :], func=ACT.Gelu_apprx_tanh) if 0 and width == N_TILE and c < 0 else nc.scalar.activation(out=gated, in_=banks_of[r][0][:], func=ACT.Gelu_apprx_tanh)
             gated_of[r] = gated
 
         def product(r):
             c, m0, per = jobs[r]
             col0, width = chunks[c]
             gated = gated_of[r]
-            nc.vector.tensor_tensor(out=gated[:], in0=banks_of[r][1][:], in1=gated[:], op=ALU.mult)
-            nc.sync.dma_start(out=act_rows[:, m0 : m0 + per, col0 : col0 + width], in_=gated[:])
+            paired = 0 and width == N_TILE and c < 0
+            bank = banks_of[r][1][:, 0, :] if paired else banks_of[r][1][:]
+            nc.vector.tensor_tensor(out=gated, in0=bank, in1=gated, op=ALU.mult)
+            if not paired:
+                nc.sync.dma_start(out=act_rows[:, m0 : m0 + per, col0 : col0 + width], in_=gated)
+            elif c % 2:
+                nc.sync.dma_start(
+                    out=act_rows[:, m0, col0 - N_TILE : col0 + N_TILE], in_=pair_of[m0][:].rearrange("p c n -> p (c n)")
+                )
 
         order = list(range(LOADS))
         loads_done = []

@@ -24,7 +24,7 @@ N_TILE = 512
 LOAD_COLS = 1024
 EPS = 1e-6
 LOADS = 12 if 0 else 2 * PASSES * (F // LOAD_COLS)
-RAW_BUFS = 8
+RAW_BUFS = 10
 TURN_COLS = 256
 
 FLOPS = 2 * TOKENS * E * (E + 2 * F)
@@ -54,7 +54,7 @@ def tile_block_pb_kernel(tc, attn, x, w_out, scale2, w_gate, w_up, out_0, out_1)
         stage = ctx.enter_context(tc.tile_pool(name="stage", bufs=2))
         code_pool = ctx.enter_context(tc.tile_pool(name="codes", bufs=3))
         work = ctx.enter_context(tc.tile_pool(name="work", bufs=4))
-        psum = ctx.enter_context(tc.psum_pool(name="psum", bufs=3 if 0 or 0 else 4))
+        psum = ctx.enter_context(tc.psum_pool(name="psum", bufs=3 if 0 or 0 or 0 else 4))
         ctx.enter_context(tc.manual_schedule())
 
         raw_of = {}
@@ -113,7 +113,7 @@ def tile_block_pb_kernel(tc, attn, x, w_out, scale2, w_gate, w_up, out_0, out_1)
 
         def vshare(u):
             width = chunks[units[u][0]][1]
-            return (448 * width // 512 if u > 1 else width) - (gshare(u) if gside(u) == 0 else 0)
+            return (416 * width // 512 if u > 1 else width) - (gshare(u) if gside(u) == 0 else 0)
 
         def regroup_gps(u):
             if u not in grouped_of:
@@ -131,13 +131,9 @@ def tile_block_pb_kernel(tc, attn, x, w_out, scale2, w_gate, w_up, out_0, out_1)
 
         def turn(rows, n0):
             bank = psum.tile([P, TURN_COLS, PACK], BF16, tag="turn", name="bank", bufs=2)
-            for first in range(0, TURN_COLS, P):
+            for t in range(PACK):
                 nc.tensor.matmul(
-                    out=bank[:, first : first + P, :],
-                    lhsT=ident_bf16[:],
-                    rhs=rows[:, :, n0 + first : n0 + first + P].rearrange("p t n -> p n t"),
-                    start=True,
-                    stop=True,
+                    out=bank[:, :, t], lhsT=ident_bf16[:], rhs=rows[:, t, n0 : n0 + TURN_COLS], start=True, stop=True
                 )
             return bank
 
@@ -168,7 +164,7 @@ def tile_block_pb_kernel(tc, attn, x, w_out, scale2, w_gate, w_up, out_0, out_1)
         def regroup_scalar(u, part=-1):
             width = chunks[units[u][0]][1]
             a, lo = vshare(u), tshare(u)
-            if part >= 0:
+            if part >= 0 and tshare(u) == 0:
                 n0 = part * 256
                 regroup(nc.scalar.copy, grouped_of[u][:, 1, n0:n0 + 256], unit_rows(u, 1)[:, :, n0:n0 + 256])
                 return
@@ -204,7 +200,9 @@ def tile_block_pb_kernel(tc, attn, x, w_out, scale2, w_gate, w_up, out_0, out_1)
         eps = const.tile([P, 1], F32)
         nc.vector.memset(eps[:], EPS)
         warm = const.tile([P, 1], F32)
-        nc.scalar.activation(out=warm[:], in_=eps[:], func=ACT.Sqrt)
+        nc.scalar.activation(out=warm[:], in_=eps[:], func=ACT.Gelu_apprx_tanh if 0 else ACT.Sqrt)
+        minus_half = const.tile([P, M_TILES], F32)
+        nc.gpsimd.memset(minus_half[:], -0.5)
 
         H = E // 2
         a_sb = keep.tile([P, M_TILES, E], BF16, align_bytes=64, tag="tokens")
@@ -223,13 +221,16 @@ def tile_block_pb_kernel(tc, attn, x, w_out, scale2, w_gate, w_up, out_0, out_1)
             nc.sync.dma_start(out=gain_row[0:1, :], in_=scale2.unsqueeze(0))
 
         gain = const.tile([P, E], F32)
+        gain_of = []
 
         def spread_gain():
             for n in range(E // N_TILE):
                 cols = slice(n * N_TILE, (n + 1) * N_TILE)
-                spread = psum.tile([P, N_TILE], F32, tag=("gate", "up")[n], name="spread")
+                spread = psum.tile([P, N_TILE], F32, tag="gain%d" % n if 0 else ("gate", "up")[n], name="spread", bufs=1 if 0 else (3 if 0 or 0 else 4))
                 nc.tensor.matmul(out=spread[:], lhsT=ones[:], rhs=gain_row[:, cols], start=True, stop=True)
-                nc.scalar.copy(out=gain[:, cols], in_=spread[:])
+                gain_of.append(spread)
+                if not 0:
+                    nc.scalar.copy(out=gain[:, cols], in_=spread[:])
 
         wo_codes = keep.tile([P, PASSES, E], U32, align_bytes=64)
         wo_scales = keep.tile([P, PASSES, E], U8, align_bytes=64)
@@ -327,14 +328,23 @@ def tile_block_pb_kernel(tc, attn, x, w_out, scale2, w_gate, w_up, out_0, out_1)
         def root_all():
             nc.scalar.activation(out=roots[:], in_=sums[:], func=ACT.Sqrt, scale=1.0 / E, bias=eps[:, 0:1])
 
+        def power_all():
+            nc.gpsimd.tensor_scalar(
+                out=roots[:], in0=sums[:], scalar1=1.0 / E, scalar2=EPS, op0=ALU.mult, op1=ALU.add
+            )
+            nc.gpsimd.tensor_tensor(out=inverse[:], in0=roots[:], in1=minus_half[:], op=ALU.pow)
+
         def reciprocal_all():
             nc.vector.reciprocal(out=inverse[:], in_=roots[:])
 
         def norm_only(m):
             hn = work.tile([P, E], BF16, tag="hn", name="hn", bufs=2)
-            nc.vector.scalar_tensor_tensor(
-                out=hn[:], in0=h_sb[:, m, :], scalar=inverse[:, m : m + 1], in1=gain[:], op0=ALU.mult, op1=ALU.mult
-            )
+            for n in range(2) if 0 else range(1):
+                cols = slice(n * N_TILE, (n + 1) * N_TILE) if 0 else slice(0, E)
+                nc.vector.scalar_tensor_tensor(
+                    out=hn[:, cols], in0=h_sb[:, m, cols], scalar=inverse[:, m : m + 1],
+                    in1=gain_of[n][:] if 0 else gain[:], op0=ALU.mult, op1=ALU.mult
+                )
             hn_of[m] = hn
 
         def store_h(m):
@@ -392,10 +402,10 @@ def tile_block_pb_kernel(tc, attn, x, w_out, scale2, w_gate, w_up, out_0, out_1)
             width = chunks[c][1]
             if 0 and width == N_TILE and c < 0:
                 if c % 2 == 0:
-                    pair_of[m0] = work.tile([P, 2, N_TILE], F32, tag="gated2", name="gated2", bufs=8 // 2)
+                    pair_of[m0] = work.tile([P, 2, N_TILE], F32, tag="gated2", name="gated2", bufs=12 // 2)
                 gated = pair_of[m0][:, c % 2]
             else:
-                single = work.tile([P, per, width], F32, tag="gated", name="gated", bufs=8 if not 0 else 4)
+                single = work.tile([P, per, width], F32, tag="gated", name="gated", bufs=12 if not 0 else 4)
                 gated = single[:]
             nc.scalar.activation(out=gated, in_=banks_of[r][0][:] if per > 1 else banks_of[r][0][:, 0, :], func=ACT.Gelu_apprx_tanh) if 0 and width == N_TILE and c < 0 else nc.scalar.activation(out=gated, in_=banks_of[r][0][:], func=ACT.Gelu_apprx_tanh)
             gated_of[r] = gated
@@ -414,7 +424,7 @@ def tile_block_pb_kernel(tc, attn, x, w_out, scale2, w_gate, w_up, out_0, out_1)
                     out=act_rows[:, m0, col0 - N_TILE : col0 + N_TILE], in_=pair_of[m0][:].rearrange("p c n -> p (c n)")
                 )
 
-        order = list(range(LOADS))
+        order = [0, 1, 3, 2] + list(range(4, LOADS))
         loads_done = []
 
         def load_next():
@@ -430,6 +440,8 @@ def tile_block_pb_kernel(tc, attn, x, w_out, scale2, w_gate, w_up, out_0, out_1)
         load_gain()
         load_x(0)
         load_x(2)
+        load_next()
+        load_next()
         load_next()
         load_next()
         load_next()
@@ -484,12 +496,13 @@ def tile_block_pb_kernel(tc, attn, x, w_out, scale2, w_gate, w_up, out_0, out_1)
         turn_norm(0)
         norm_only(1)
         turn_norm(1)
+        open_unit(1)
+        regroup_scalar(1)
         norm_only(2)
         turn_norm(2)
         norm_only(3)
         turn_norm(3)
         regroup_vector(1)
-        regroup_scalar(1)
         quantise_unit(0)
         quantise_norm(0)
         quantise_norm(1)
@@ -508,11 +521,11 @@ def tile_block_pb_kernel(tc, attn, x, w_out, scale2, w_gate, w_up, out_0, out_1)
                 regroup_vector(i)
             if i <= nu:
                 quantise_unit(i - 1)
+            load_next()
             for r in mult.get(i - 2, []):
                 product(r)
             if i + 1 < nu:
                 regroup_gps(i + 1)
-            load_next()
             if i < nu:
                 copy_turned(i)
             if i < nu:

@@ -24,7 +24,7 @@ N_TILE = 512
 LOAD_COLS = 1024
 EPS = 1e-6
 LOADS = 12 if 0 else 2 * PASSES * (F // LOAD_COLS)
-RAW_BUFS = 10
+RAW_BUFS = 9
 TURN_COLS = 256
 
 FLOPS = 2 * TOKENS * E * (E + 2 * F)
@@ -113,7 +113,7 @@ def tile_block_pb_kernel(tc, attn, x, w_out, scale2, w_gate, w_up, out_0, out_1)
 
         def vshare(u):
             width = chunks[units[u][0]][1]
-            return (416 * width // 512 if u > 1 else width) - (gshare(u) if gside(u) == 0 else 0)
+            return (424 * width // 512 // 8 * 8 if u > 1 else width) - (gshare(u) if gside(u) == 0 else 0)
 
         def regroup_gps(u):
             if u not in grouped_of:
@@ -145,6 +145,8 @@ def tile_block_pb_kernel(tc, attn, x, w_out, scale2, w_gate, w_up, out_0, out_1)
             grouped_of[u] = stage.tile([P, 2, width, PACK], BF16, align_bytes=64, tag="grouped", name="grouped")
 
         def upshare(u):
+            if 0 and 2 <= u <= 2:
+                return 0
             return 0 * chunks[units[u][0]][1] // 512 if u > 2 else 0
 
         def regroup_vector(u):
@@ -226,7 +228,7 @@ def tile_block_pb_kernel(tc, attn, x, w_out, scale2, w_gate, w_up, out_0, out_1)
         def spread_gain():
             for n in range(E // N_TILE):
                 cols = slice(n * N_TILE, (n + 1) * N_TILE)
-                spread = psum.tile([P, N_TILE], F32, tag="gain%d" % n if 0 else ("gate", "up")[n], name="spread", bufs=1 if 0 else (3 if 0 or 0 else 4))
+                spread = psum.tile([P, N_TILE], F32, tag="gain%d" % n if 0 else ("gate", "up")[n], name="spread")
                 nc.tensor.matmul(out=spread[:], lhsT=ones[:], rhs=gain_row[:, cols], start=True, stop=True)
                 gain_of.append(spread)
                 if not 0:
@@ -256,7 +258,7 @@ def tile_block_pb_kernel(tc, attn, x, w_out, scale2, w_gate, w_up, out_0, out_1)
                 wo_grouped[g] = stage.tile([P, E, PACK], BF16, align_bytes=64, tag="grouped", name="grouped")
             width = H if n < 2 else E
             first = H if n == 1 else 0
-            cut = (320, 320, 640)[n]
+            cut = (352, 352, 704)[n]
             rows = wo_raw[(n, g)]
             grouped = wo_grouped[g][:, first : first + width]
             regroup(nc.vector.tensor_copy, grouped[:, 0:cut], rows[:, :, 0:cut])
@@ -328,6 +330,14 @@ def tile_block_pb_kernel(tc, attn, x, w_out, scale2, w_gate, w_up, out_0, out_1)
         def root_all():
             nc.scalar.activation(out=roots[:], in_=sums[:], func=ACT.Sqrt, scale=1.0 / E, bias=eps[:, 0:1])
 
+        def root_pair(k):
+            two = slice(2 * k, 2 * k + 2)
+            nc.scalar.activation(out=roots[:, two], in_=sums[:, two], func=ACT.Sqrt, scale=1.0 / E, bias=eps[:, 0:1])
+
+        def reciprocal_pair(k):
+            two = slice(2 * k, 2 * k + 2)
+            nc.vector.reciprocal(out=inverse[:, two], in_=roots[:, two])
+
         def power_all():
             nc.gpsimd.tensor_scalar(
                 out=roots[:], in0=sums[:], scalar1=1.0 / E, scalar2=EPS, op0=ALU.mult, op1=ALU.add
@@ -372,7 +382,7 @@ def tile_block_pb_kernel(tc, attn, x, w_out, scale2, w_gate, w_up, out_0, out_1)
 
         jobs = []
         for c, (col0, width) in enumerate(chunks):
-            per = N_TILE // width
+            per = N_TILE // width if not (1 and c == len(chunks) - 1) else 1
             for m0 in range(0, M_TILES, per):
                 jobs.append((c, m0, per))
 
@@ -405,7 +415,7 @@ def tile_block_pb_kernel(tc, attn, x, w_out, scale2, w_gate, w_up, out_0, out_1)
                     pair_of[m0] = work.tile([P, 2, N_TILE], F32, tag="gated2", name="gated2", bufs=12 // 2)
                 gated = pair_of[m0][:, c % 2]
             else:
-                single = work.tile([P, per, width], F32, tag="gated", name="gated", bufs=12 if not 0 else 4)
+                single = work.tile([P, per, width], F32, tag="gated", name="gated", bufs=12 if not 0 else 6)
                 gated = single[:]
             nc.scalar.activation(out=gated, in_=banks_of[r][0][:] if per > 1 else banks_of[r][0][:, 0, :], func=ACT.Gelu_apprx_tanh) if 0 and width == N_TILE and c < 0 else nc.scalar.activation(out=gated, in_=banks_of[r][0][:], func=ACT.Gelu_apprx_tanh)
             gated_of[r] = gated
@@ -424,7 +434,7 @@ def tile_block_pb_kernel(tc, attn, x, w_out, scale2, w_gate, w_up, out_0, out_1)
                     out=act_rows[:, m0, col0 - N_TILE : col0 + N_TILE], in_=pair_of[m0][:].rearrange("p c n -> p (c n)")
                 )
 
-        order = [0, 1, 3, 2] + list(range(4, LOADS))
+        order = ([0, 1, 2, 3] if 0 else [0, 1, 3, 2]) + list(range(4, LOADS))
         loads_done = []
 
         def load_next():
@@ -440,7 +450,6 @@ def tile_block_pb_kernel(tc, attn, x, w_out, scale2, w_gate, w_up, out_0, out_1)
         load_gain()
         load_x(0)
         load_x(2)
-        load_next()
         load_next()
         load_next()
         load_next()
@@ -476,6 +485,7 @@ def tile_block_pb_kernel(tc, attn, x, w_out, scale2, w_gate, w_up, out_0, out_1)
         add(1, 1)
         store_h(1)
         square_only(1)
+        root_pair(0)
         project(2, 0)
         project(2, 1)
         add(2, 0)
@@ -488,14 +498,15 @@ def tile_block_pb_kernel(tc, attn, x, w_out, scale2, w_gate, w_up, out_0, out_1)
         add(3, 1)
         store_h(3)
         square_only(3)
-        root_all()
+        root_pair(1)
         regroup_vector(0)
         regroup_scalar(0)
-        reciprocal_all()
+        reciprocal_pair(0)
         norm_only(0)
         turn_norm(0)
         norm_only(1)
         turn_norm(1)
+        reciprocal_pair(1)
         open_unit(1)
         regroup_scalar(1)
         norm_only(2)

@@ -23,7 +23,8 @@ PASSES = E // K_PASS
 N_TILE = 512
 LOAD_COLS = 1024
 EPS = 1e-6
-LOADS = 12 if 0 else 2 * PASSES * (F // LOAD_COLS)
+SPANS = [0, 1024, 2048, 3072, 4096]
+LOADS = 4 * (len(SPANS) - 1) if 0 else 12 if 0 else 2 * PASSES * (F // LOAD_COLS)
 RAW_BUFS = 9
 TURN_COLS = 256
 
@@ -80,7 +81,17 @@ def tile_block_pb_kernel(tc, attn, x, w_out, scale2, w_gate, w_up, out_0, out_1)
                 for q in (2, 3):
                     raw_of[(w, g, q)] = raw[:, :, (q - 2) * LOAD_COLS : (q - 1) * LOAD_COLS]
 
+        def load_span(k):
+            s, rest = divmod(k, 2 * PASSES)
+            g, w = divmod(rest, 2)
+            first, last = SPANS[s], SPANS[s + 1]
+            raw = raw_pool.tile([P, PACK, last - first], BF16, tag="raw", name="raw_w")
+            nc.sync.dma_start(out=raw[:], in_=(gate_w, up_w)[w][g][:, :, first:last])
+            raw_of[(w, g, s)] = raw
+
         def load_weights(k):
+            if 0:
+                return load_span(k)
             if 0:
                 return load_big(k)
             q, rest = divmod(k, 2 * PASSES)
@@ -100,6 +111,9 @@ def tile_block_pb_kernel(tc, attn, x, w_out, scale2, w_gate, w_up, out_0, out_1)
             c, g = units[u]
             col0, width = chunks[c]
             q, n0 = divmod(col0, LOAD_COLS)
+            if 0:
+                q = max(s for s in range(len(SPANS) - 1) if SPANS[s] <= col0)
+                n0 = col0 - SPANS[q]
             return raw_of[(w, g, q)][:, :, n0 : n0 + width]
 
         def tshare(u):
@@ -113,7 +127,7 @@ def tile_block_pb_kernel(tc, attn, x, w_out, scale2, w_gate, w_up, out_0, out_1)
 
         def vshare(u):
             width = chunks[units[u][0]][1]
-            return (424 * width // 512 // 8 * 8 if u > 1 else width) - (gshare(u) if gside(u) == 0 else 0)
+            return (400 * width // 512 // 8 * 8 if u > 1 else width) - (gshare(u) if gside(u) == 0 else 0)
 
         def regroup_gps(u):
             if u not in grouped_of:
@@ -202,7 +216,7 @@ def tile_block_pb_kernel(tc, attn, x, w_out, scale2, w_gate, w_up, out_0, out_1)
         eps = const.tile([P, 1], F32)
         nc.vector.memset(eps[:], EPS)
         warm = const.tile([P, 1], F32)
-        nc.scalar.activation(out=warm[:], in_=eps[:], func=ACT.Gelu_apprx_tanh if 0 else ACT.Sqrt)
+        nc.scalar.activation(out=warm[:], in_=eps[:], func=ACT.Gelu_apprx_tanh if 1 else ACT.Sqrt)
         minus_half = const.tile([P, M_TILES], F32)
         nc.gpsimd.memset(minus_half[:], -0.5)
 
@@ -337,6 +351,13 @@ def tile_block_pb_kernel(tc, attn, x, w_out, scale2, w_gate, w_up, out_0, out_1)
         def reciprocal_pair(k):
             two = slice(2 * k, 2 * k + 2)
             nc.vector.reciprocal(out=inverse[:, two], in_=roots[:, two])
+
+        def power_pair(k):
+            two = slice(2 * k, 2 * k + 2)
+            nc.gpsimd.tensor_scalar(
+                out=roots[:, two], in0=sums[:, two], scalar1=1.0 / E, scalar2=EPS, op0=ALU.mult, op1=ALU.add
+            )
+            nc.gpsimd.tensor_tensor(out=inverse[:, two], in0=roots[:, two], in1=minus_half[:, two], op=ALU.pow)
 
         def power_all():
             nc.gpsimd.tensor_scalar(
@@ -477,36 +498,30 @@ def tile_block_pb_kernel(tc, attn, x, w_out, scale2, w_gate, w_up, out_0, out_1)
         project(0, 1)
         add(0, 0)
         add(0, 1)
-        store_h(0)
         square_only(0)
         project(1, 0)
         project(1, 1)
         add(1, 0)
         add(1, 1)
-        store_h(1)
         square_only(1)
-        root_pair(0)
+        power_pair(0)
         project(2, 0)
         project(2, 1)
         add(2, 0)
         add(2, 1)
-        store_h(2)
         square_only(2)
         project(3, 0)
         project(3, 1)
         add(3, 0)
         add(3, 1)
-        store_h(3)
         square_only(3)
-        root_pair(1)
+        power_pair(1)
         regroup_vector(0)
         regroup_scalar(0)
-        reciprocal_pair(0)
         norm_only(0)
         turn_norm(0)
         norm_only(1)
         turn_norm(1)
-        reciprocal_pair(1)
         open_unit(1)
         regroup_scalar(1)
         norm_only(2)
@@ -535,6 +550,8 @@ def tile_block_pb_kernel(tc, attn, x, w_out, scale2, w_gate, w_up, out_0, out_1)
             load_next()
             for r in mult.get(i - 2, []):
                 product(r)
+            if 9 <= i < 13:
+                store_h(i - 9)
             if i + 1 < nu:
                 regroup_gps(i + 1)
             if i < nu:

@@ -10,28 +10,42 @@ U8 = mybir.dt.uint8
 FP8X4 = mybir.dt.float8_e4m3fn_x4
 ACT = mybir.ActivationFunctionType
 ALU = mybir.AluOpType
-WIDTHS = (512, 512, 512, 512, 512, 512, 512, 256, 256)
 
 P = 128
 PACK = 4
 K_PASS = P * PACK
 TOKENS = 512
+M_TILES = TOKENS // P
 E = 1024
 F = 4096
-M_TILES = TOKENS // P
 PASSES = E // K_PASS
 N_TILE = 512
-LOAD_COLS = 1024
+HALF = E // 2
 EPS = 1e-6
-SPANS = [0, 1024, 2048, 3072, 4096]
-LOADS = 4 * (len(SPANS) - 1) if 0 else 12 if 0 else 2 * PASSES * (F // LOAD_COLS)
+
+LOAD_COLS = 1024
+LOADS = 2 * PASSES * (F // LOAD_COLS)
+FIRST_LOADS = (0, 1, 3, 2)
+
+WIDTHS = (512,) * 7 + (256, 256)
+UNITS = len(WIDTHS) * PASSES
+
+OUT_VECTOR_COLS = {HALF: 352, E: 704}
+GATE_VECTOR_COLS = {512: 408, 256: 168}
+WHOLE_GATE_UNITS = 2
+UP_VECTOR_COLS = 96
+UP_VECTOR_UNITS = (3, 4)
+UP_GPSIMD_COLS = 128
+FIRST_GPSIMD_UNIT = 5
+H_STORES = 9
+
 RAW_BUFS = 9
-TURN_COLS = 256
+ACT_BUFS = 12
 
 FLOPS = 2 * TOKENS * E * (E + 2 * F)
 
 
-def regroup(copy, grouped, rows):
+def interleave(copy, grouped, rows):
     copy(
         out=grouped.rearrange("p (c i) t -> p c t i", i=4),
         in_=rows.rearrange("p t (c i) -> p c t i", i=4),
@@ -40,163 +54,182 @@ def regroup(copy, grouped, rows):
 
 def tile_block_pb_kernel(tc, attn, x, w_out, scale2, w_gate, w_up, out_0, out_1):
     nc = tc.nc
-    attn_rows = attn.rearrange("b s i d -> (b s) (i d)").rearrange("(p m) e -> p m e", p=P)
-    x_rows = x.rearrange("b s e -> (b s) e").rearrange("(p m) e -> p m e", p=P)
-    h_rows = out_0.rearrange("b s e -> (b s) e").rearrange("(p m) e -> p m e", p=P)
-    act_rows = out_1.rearrange("b s f -> (b s) f").rearrange("(p m) f -> p m f", p=P)
-    out_w = w_out.rearrange("i d e -> (i d) e").rearrange("(g p t) n -> g p t n", t=PACK, p=P)
-    gate_w = w_gate.rearrange("(g p t) n -> g p t n", t=PACK, p=P)
-    up_w = w_up.rearrange("(g p t) n -> g p t n", t=PACK, p=P)
+    attn_tokens = attn.rearrange("b s i d -> (b s) (i d)").rearrange("(p m) k -> p m k", p=P)
+    x_tokens = x.rearrange("b s e -> (b s) e").rearrange("(p m) e -> p m e", p=P)
+    h_tokens = out_0.rearrange("b s e -> (b s) e").rearrange("(p m) e -> p m e", p=P)
+    act_tokens = out_1.rearrange("b s f -> (b s) f").rearrange("(p m) f -> p m f", p=P)
+    w_out_rows = w_out.rearrange("i d e -> (i d) e").rearrange("(g p t) n -> g p t n", t=PACK, p=P)
+    gate_up_rows = [w.rearrange("(g p t) n -> g p t n", t=PACK, p=P) for w in (w_gate, w_up)]
 
     with ExitStack() as ctx:
         const = ctx.enter_context(tc.tile_pool(name="const", bufs=1))
         keep = ctx.enter_context(tc.tile_pool(name="keep", bufs=1))
         raw_pool = ctx.enter_context(tc.tile_pool(name="raw", bufs=RAW_BUFS))
-        stage = ctx.enter_context(tc.tile_pool(name="stage", bufs=2))
+        grouped_pool = ctx.enter_context(tc.tile_pool(name="grouped", bufs=2))
         code_pool = ctx.enter_context(tc.tile_pool(name="codes", bufs=3))
-        work = ctx.enter_context(tc.tile_pool(name="work", bufs=4))
-        psum = ctx.enter_context(tc.psum_pool(name="psum", bufs=3 if 0 or 0 or 0 else 4))
+        work = ctx.enter_context(tc.tile_pool(name="work", bufs=2))
+        psum = ctx.enter_context(tc.psum_pool(name="psum", bufs=4))
         ctx.enter_context(tc.manual_schedule())
 
-        raw_of = {}
-        grouped_of = {}
-        codes_of = {}
-        banks_of = {}
-        gated_of = {}
-        turned_of = {}
+        ident = const.tile([P, P], F32)
+        make_identity(nc, ident[:])
+        gain_row = const.tile([P, E], BF16)
+        nc.gpsimd.memset(gain_row[:], 0.0)
+        minus_half = const.tile([P, M_TILES], F32)
+        nc.gpsimd.memset(minus_half[:], -0.5)
+        ones = const.tile([P, P], BF16)
+        nc.vector.memset(ones[:], 1.0)
+        warm = const.tile([P, 1], F32)
+        nc.scalar.activation(out=warm[:], in_=ones[:, 0:1], func=ACT.Gelu_apprx_tanh)
 
-        def load_big(k):
-            if k < 8:
-                q, rest = divmod(k, 2 * PASSES)
-                g, w = divmod(rest, 2)
-                if g == 0:
-                    raw_of[(w, q)] = raw_pool.tile([P, PASSES, PACK, LOAD_COLS], BF16, tag="raw", name="raw_w")
-                raw = raw_of[(w, q)][:, g]
-                nc.sync.dma_start(out=raw, in_=(gate_w, up_w)[w][g][:, :, q * LOAD_COLS : (q + 1) * LOAD_COLS])
-                raw_of[(w, g, q)] = raw
-            else:
-                g, w = divmod(k - 8, 2)
-                raw = raw_pool.tile([P, PACK, 2 * LOAD_COLS], BF16, tag="raw", name="raw_b")
-                nc.sync.dma_start(out=raw[:], in_=(gate_w, up_w)[w][g][:, :, 2 * LOAD_COLS : F])
-                for q in (2, 3):
-                    raw_of[(w, g, q)] = raw[:, :, (q - 2) * LOAD_COLS : (q - 1) * LOAD_COLS]
+        w_out_raw = {}
 
-        def load_span(k):
-            s, rest = divmod(k, 2 * PASSES)
-            g, w = divmod(rest, 2)
-            first, last = SPANS[s], SPANS[s + 1]
-            raw = raw_pool.tile([P, PACK, last - first], BF16, tag="raw", name="raw_w")
-            nc.sync.dma_start(out=raw[:], in_=(gate_w, up_w)[w][g][:, :, first:last])
-            raw_of[(w, g, s)] = raw
+        def load_w_out(g, first, width):
+            raw = raw_pool.tile([P, PACK, width], BF16, tag="raw", name="raw_o")
+            nc.sync.dma_start(out=raw[:], in_=w_out_rows[g][:, :, first : first + width])
+            w_out_raw[(g, first)] = raw
+
+        gate_up_raw = {}
+        load_order = FIRST_LOADS + tuple(range(len(FIRST_LOADS), LOADS))
 
         def load_weights(k):
-            if 0:
-                return load_span(k)
-            if 0:
-                return load_big(k)
-            q, rest = divmod(k, 2 * PASSES)
+            q, rest = divmod(load_order[k], 2 * PASSES)
             g, w = divmod(rest, 2)
             raw = raw_pool.tile([P, PACK, LOAD_COLS], BF16, tag="raw", name="raw_w")
-            nc.sync.dma_start(out=raw[:], in_=(gate_w, up_w)[w][g][:, :, q * LOAD_COLS : (q + 1) * LOAD_COLS])
-            raw_of[(w, g, q)] = raw
+            nc.sync.dma_start(out=raw[:], in_=gate_up_rows[w][g][:, :, q * LOAD_COLS : (q + 1) * LOAD_COLS])
+            gate_up_raw[(w, g, q)] = raw
 
-        chunks = []
-        col0 = 0
-        for width in WIDTHS:
-            chunks.append((col0, width))
-            col0 += width
-        units = [(c, g) for c in range(len(chunks)) for g in range(PASSES)]
+        load_w_out(0, 0, HALF)
+        load_w_out(0, HALF, HALF)
+        load_w_out(1, 0, E)
+        attn_sb = keep.tile([P, M_TILES, E], BF16)
+        for m in range(0, M_TILES, 2):
+            nc.sync.dma_start(out=attn_sb[:, m : m + 2, :], in_=attn_tokens[:, m : m + 2, :])
+        nc.sync.dma_start(out=gain_row[0:1, :], in_=scale2.unsqueeze(0))
+        x_sb = keep.tile([P, M_TILES, E], BF16)
+        for m in range(0, M_TILES, 2):
+            nc.sync.dma_start(out=x_sb[:, m : m + 2, :], in_=x_tokens[:, m : m + 2, :])
+        free_bufs = RAW_BUFS - len(w_out_raw)
+        for k in range(free_bufs):
+            load_weights(k)
+
+        w_out_codes = keep.tile([P, PASSES, E], U32, align_bytes=64)
+        w_out_scales = keep.tile([P, PASSES, E], U8, align_bytes=64)
+        w_out_grouped = {}
+
+        def interleave_w_out(g, first, width):
+            if first == 0:
+                w_out_grouped[g] = grouped_pool.tile([P, E, PACK], BF16, align_bytes=64, tag="grouped", name="grouped")
+            grouped = w_out_grouped[g][:, first : first + width]
+            rows = w_out_raw[(g, first)]
+            cut = OUT_VECTOR_COLS[width]
+            interleave(nc.vector.tensor_copy, grouped[:, 0:cut], rows[:, :, 0:cut])
+            interleave(nc.scalar.copy, grouped[:, cut:width], rows[:, :, cut:width])
+
+        def quantise_w_out(g):
+            nc.vector.quantize_mx(
+                out=w_out_codes[:, g].bitcast(FP8X4),
+                scales=w_out_scales[:, g],
+                in_=w_out_grouped[g][:].rearrange("p n t -> p (n t)"),
+            )
+
+        def transpose_tokens(values, grouped, m):
+            words = values.bitcast(F32)
+            words_t = psum.tile([P, PASSES, 2, P], F32, tag=("gate", "up")[m % 2], name="words_t")
+            for g in range(PASSES):
+                for v in range(2):
+                    first = 2 * g * P + v
+                    nc.tensor.transpose(words_t[:, g, v, :], words[:, first : 2 * (g + 1) * P : 2], ident[:])
+            nc.scalar.copy(
+                out=grouped.bitcast(F32).rearrange("p (g r v) -> p g r v", g=PASSES, v=2),
+                in_=words_t[:].rearrange("p g v r -> p g r v"),
+            )
+
+        def quantise_tokens(grouped, codes, scales, m):
+            nc.vector.quantize_mx(
+                out=codes[:, m].rearrange("p g r -> p (g r)").bitcast(FP8X4),
+                scales=scales[:, m].rearrange("p g r -> p (g r)"),
+                in_=grouped[:, m, :],
+            )
+
+        attn_grouped = keep.tile([P, M_TILES, PASSES * P * PACK], BF16, align_bytes=64)
+        attn_codes = keep.tile([P, M_TILES, PASSES, P], U32, align_bytes=64)
+        attn_scales = keep.tile([P, M_TILES, PASSES, P], U8, align_bytes=64)
+
+        interleave_w_out(0, 0, HALF)
+        interleave_w_out(0, HALF, HALF)
+        quantise_w_out(0)
+        interleave_w_out(1, 0, E)
+        for m in range(M_TILES):
+            transpose_tokens(attn_sb[:, m, :], attn_grouped[:, m, :], m)
+        quantise_w_out(1)
+        for m in range(M_TILES):
+            quantise_tokens(attn_grouped, attn_codes, attn_scales, m)
+
+        gain = const.tile([P, E], F32)
+        for n in range(E // N_TILE):
+            cols = slice(n * N_TILE, (n + 1) * N_TILE)
+            spread = psum.tile([P, N_TILE], F32, tag=("gate", "up")[n], name="spread")
+            nc.tensor.matmul(out=spread[:], lhsT=ones[:], rhs=gain_row[:, cols], start=True, stop=True)
+            nc.scalar.copy(out=gain[:, cols], in_=spread[:])
+        for k in range(free_bufs, RAW_BUFS):
+            load_weights(k)
+
+        first_cols = [sum(WIDTHS[:c]) for c in range(len(WIDTHS))]
+        grouped_of = {}
+        codes_of = {}
 
         def unit_rows(u, w):
-            c, g = units[u]
-            col0, width = chunks[c]
-            q, n0 = divmod(col0, LOAD_COLS)
-            if 0:
-                q = max(s for s in range(len(SPANS) - 1) if SPANS[s] <= col0)
-                n0 = col0 - SPANS[q]
-            return raw_of[(w, g, q)][:, :, n0 : n0 + width]
+            c, g = divmod(u, PASSES)
+            q, first = divmod(first_cols[c], LOAD_COLS)
+            return gate_up_raw[(w, g, q)][:, :, first : first + WIDTHS[c]]
 
-        def tshare(u):
-            return min(0, chunks[units[u][0]][1]) if u < 99 else 0
-
-        def gshare(u):
-            return 128 * chunks[units[u][0]][1] // 512 if u > 2 else 0
-
-        def gside(u):
-            return (u % 2, 1, 0)[1]
-
-        def vshare(u):
-            width = chunks[units[u][0]][1]
-            return (400 * width // 512 // 8 * 8 if u > 1 else width) - (gshare(u) if gside(u) == 0 else 0)
-
-        def regroup_gps(u):
+        def unit_grouped(u):
             if u not in grouped_of:
-                open_unit(u)
-            share, width, w = gshare(u), chunks[units[u][0]][1], gside(u)
-            if share:
-                nc.gpsimd.tensor_scalar(
-                    out=grouped_of[u][:, w, width - share :, :],
-                    in0=unit_rows(u, w)[:, :, width - share :].rearrange("p t n -> p n t"),
-                    scalar1=1.0,
-                    scalar2=0.0,
-                    op0=ALU.mult,
-                    op1=ALU.add,
+                width = WIDTHS[u // PASSES]
+                grouped_of[u] = grouped_pool.tile(
+                    [P, 2, width, PACK], BF16, align_bytes=64, tag="grouped", name="grouped"
                 )
+            return grouped_of[u]
 
-        def turn(rows, n0):
-            bank = psum.tile([P, TURN_COLS, PACK], BF16, tag="turn", name="bank", bufs=2)
-            for t in range(PACK):
-                nc.tensor.matmul(
-                    out=bank[:, :, t], lhsT=ident_bf16[:], rhs=rows[:, t, n0 : n0 + TURN_COLS], start=True, stop=True
-                )
-            return bank
+        def gate_cut(u):
+            width = WIDTHS[u // PASSES]
+            return width if u < WHOLE_GATE_UNITS else GATE_VECTOR_COLS[width]
 
-        def turn_unit(u):
-            turned_of[u] = [(n0, turn(unit_rows(u, 1), n0)) for n0 in range(0, tshare(u), TURN_COLS)]
+        def up_cut(u):
+            width = WIDTHS[u // PASSES]
+            if u in UP_VECTOR_UNITS:
+                return width - UP_VECTOR_COLS
+            return width - UP_GPSIMD_COLS if u >= FIRST_GPSIMD_UNIT else width
 
-        def open_unit(u):
-            width = chunks[units[u][0]][1]
-            grouped_of[u] = stage.tile([P, 2, width, PACK], BF16, align_bytes=64, tag="grouped", name="grouped")
+        def interleave_vector(u):
+            grouped = unit_grouped(u)
+            interleave(nc.vector.tensor_copy, grouped[:, 0, 0 : gate_cut(u)], unit_rows(u, 0)[:, :, 0 : gate_cut(u)])
+            if u in UP_VECTOR_UNITS:
+                interleave(nc.vector.tensor_copy, grouped[:, 1, up_cut(u) :], unit_rows(u, 1)[:, :, up_cut(u) :])
 
-        def upshare(u):
-            if 0 and 2 <= u <= 2:
-                return 0
-            return 0 * chunks[units[u][0]][1] // 512 if u > 2 else 0
+        def interleave_scalar(u):
+            grouped = unit_grouped(u)
+            interleave(nc.scalar.copy, grouped[:, 1, 0 : up_cut(u)], unit_rows(u, 1)[:, :, 0 : up_cut(u)])
+            if gate_cut(u) < WIDTHS[u // PASSES]:
+                interleave(nc.scalar.copy, grouped[:, 0, gate_cut(u) :], unit_rows(u, 0)[:, :, gate_cut(u) :])
 
-        def regroup_vector(u):
-            if u not in grouped_of:
-                open_unit(u)
-            a, width, b = vshare(u), chunks[units[u][0]][1], upshare(u)
-            if 0 and gshare(u):
-                a += 8
-            regroup(nc.vector.tensor_copy, grouped_of[u][:, 0, 0:a], unit_rows(u, 0)[:, :, 0:a])
-            if b:
-                regroup(nc.vector.tensor_copy, grouped_of[u][:, 1, width - b :], unit_rows(u, 1)[:, :, width - b :])
-
-        def copy_turned(u):
-            for n0, bank in turned_of.get(u, []):
-                nc.scalar.copy(out=grouped_of[u][:, 1, n0 : n0 + TURN_COLS, :], in_=bank[:])
-
-        def regroup_scalar(u, part=-1):
-            width = chunks[units[u][0]][1]
-            a, lo = vshare(u), tshare(u)
-            if part >= 0 and tshare(u) == 0:
-                n0 = part * 256
-                regroup(nc.scalar.copy, grouped_of[u][:, 1, n0:n0 + 256], unit_rows(u, 1)[:, :, n0:n0 + 256])
-                return
-            up_end = width - (gshare(u) if gside(u) else 0) - upshare(u)
-            gate_end = width - (0 if gside(u) else gshare(u))
-            if up_end > lo:
-                regroup(nc.scalar.copy, grouped_of[u][:, 1, lo:up_end], unit_rows(u, 1)[:, :, lo:up_end])
-            if a < gate_end:
-                regroup(nc.scalar.copy, grouped_of[u][:, 0, a:gate_end], unit_rows(u, 0)[:, :, a:gate_end])
+        def interleave_gpsimd(u):
+            nc.gpsimd.tensor_scalar(
+                out=unit_grouped(u)[:, 1, up_cut(u) :, :],
+                in0=unit_rows(u, 1)[:, :, up_cut(u) :].rearrange("p t n -> p n t"),
+                scalar1=1.0,
+                scalar2=0.0,
+                op0=ALU.mult,
+                op1=ALU.add,
+            )
 
         def quantise_unit(u):
-            c, g = units[u]
-            width = chunks[c][1]
+            c, g = divmod(u, PASSES)
             if g == 0:
-                w_codes = code_pool.tile([P, PASSES, 2, width], U32, align_bytes=64, tag="w_codes", name="w_codes")
-                w_scales = code_pool.tile([P, PASSES, 2, width], U8, align_bytes=64, tag="w_scales", name="w_scales")
+                shape = [P, PASSES, 2, WIDTHS[c]]
+                w_codes = code_pool.tile(shape, U32, align_bytes=64, tag="w_codes", name="w_codes")
+                w_scales = code_pool.tile(shape, U8, align_bytes=64, tag="w_scales", name="w_scales")
                 codes_of[c] = (w_codes, w_scales)
             w_codes, w_scales = codes_of[c]
             nc.vector.quantize_mx(
@@ -205,362 +238,113 @@ def tile_block_pb_kernel(tc, attn, x, w_out, scale2, w_gate, w_up, out_0, out_1)
                 in_=grouped_of[u][:].rearrange("p w n t -> p (w n t)"),
             )
 
-        ident_bf16 = const.tile([P, P], BF16)
-        if 0 or 0: make_identity(nc, ident_bf16[:])
-        ident_f32 = const.tile([P, P], F32)
-        make_identity(nc, ident_f32[:])
-        gain_row = const.tile([P, E], BF16)
-        nc.gpsimd.memset(gain_row[:], 0.0)
-        ones = const.tile([P, P], BF16)
-        nc.vector.memset(ones[:], 1.0)
-        eps = const.tile([P, 1], F32)
-        nc.vector.memset(eps[:], EPS)
-        warm = const.tile([P, 1], F32)
-        nc.scalar.activation(out=warm[:], in_=eps[:], func=ACT.Gelu_apprx_tanh if 1 else ACT.Sqrt)
-        minus_half = const.tile([P, M_TILES], F32)
-        nc.gpsimd.memset(minus_half[:], -0.5)
-
-        H = E // 2
-        a_sb = keep.tile([P, M_TILES, E], BF16, align_bytes=64, tag="tokens")
-        x_sb = keep.tile([P, M_TILES, E], BF16)
-        wo_raw = {}
-
-        def load_out(n, g):
-            width = H if n < 2 else E
-            first = H if n == 1 else 0
-            wo_raw[(n, g)] = raw_pool.tile([P, PACK, width], BF16, tag="raw", name="raw_o")
-            nc.sync.dma_start(out=wo_raw[(n, g)][:], in_=out_w[g][:, :, first : first + width])
-
-        def load_attn(m): nc.sync.dma_start(out=a_sb[:, m : m + 2, :], in_=attn_rows[:, m : m + 2, :])
-        def load_x(m): nc.sync.dma_start(out=x_sb[:, m : m + 2, :], in_=x_rows[:, m : m + 2, :])
-        def load_gain():
-            nc.sync.dma_start(out=gain_row[0:1, :], in_=scale2.unsqueeze(0))
-
-        gain = const.tile([P, E], F32)
-        gain_of = []
-
-        def spread_gain():
+        h_sb = keep.tile([P, M_TILES, E], F32)
+        sums = keep.tile([P, M_TILES], F32)
+        means = keep.tile([P, M_TILES], F32)
+        rstd = keep.tile([P, M_TILES], F32)
+        for m in range(M_TILES):
             for n in range(E // N_TILE):
                 cols = slice(n * N_TILE, (n + 1) * N_TILE)
-                spread = psum.tile([P, N_TILE], F32, tag="gain%d" % n if 0 else ("gate", "up")[n], name="spread")
-                nc.tensor.matmul(out=spread[:], lhsT=ones[:], rhs=gain_row[:, cols], start=True, stop=True)
-                gain_of.append(spread)
-                if not 0:
-                    nc.scalar.copy(out=gain[:, cols], in_=spread[:])
+                acc = psum.tile([P, N_TILE], F32, tag=("gate", "up")[m % 2], name="acc")
+                for g in range(PASSES):
+                    nc.tensor.matmul_mx(
+                        out=acc[:],
+                        lhsT=attn_codes[:, m, g, :].bitcast(FP8X4),
+                        lhsT_scale=attn_scales[:, m, g, :],
+                        rhs=w_out_codes[:, g, cols].bitcast(FP8X4),
+                        rhs_scale=w_out_scales[:, g, cols],
+                        start=(g == 0),
+                        stop=(g == PASSES - 1),
+                    )
+                nc.vector.tensor_tensor(out=h_sb[:, m, cols], in0=acc[:], in1=x_sb[:, m, cols], op=ALU.add)
+            squares = work.tile([P, E], BF16, tag="squares", name="squares")
+            nc.scalar.activation(out=squares[:], in_=h_sb[:, m, :], func=ACT.Square, accum_out=sums[:, m : m + 1])
+            if m % 2 == 1:
+                two = slice(m - 1, m + 1)
+                nc.gpsimd.tensor_scalar(
+                    out=means[:, two], in0=sums[:, two], scalar1=1.0 / E, scalar2=EPS, op0=ALU.mult, op1=ALU.add
+                )
+                nc.gpsimd.tensor_tensor(out=rstd[:, two], in0=means[:, two], in1=minus_half[:, two], op=ALU.pow)
 
-        wo_codes = keep.tile([P, PASSES, E], U32, align_bytes=64)
-        wo_scales = keep.tile([P, PASSES, E], U8, align_bytes=64)
-        a_grouped = keep.tile([P, M_TILES, PASSES * P * PACK], BF16, align_bytes=64)
-        a_codes = keep.tile([P, M_TILES, PASSES, P], U32, align_bytes=64)
-        a_scales = keep.tile([P, M_TILES, PASSES, P], U8, align_bytes=64)
-
-        def transpose_words(words, words_t):
-            for g in range(PASSES):
-                for u in range(2):
-                    w0 = 2 * g * P
-                    nc.tensor.transpose(words_t[:, g, u, :], words[:, w0 + u : w0 + 2 * P : 2], ident_f32[:])
-
-        def words_out(grouped, words_t):
-            nc.scalar.copy(
-                out=grouped.bitcast(F32).rearrange("p (g r u) -> p g r u", g=PASSES, u=2),
-                in_=words_t[:].rearrange("p g u r -> p g r u"),
-            )
-
-        wo_grouped = {}
-        def regroup_out(n, g):
-            if n != 1:
-                wo_grouped[g] = stage.tile([P, E, PACK], BF16, align_bytes=64, tag="grouped", name="grouped")
-            width = H if n < 2 else E
-            first = H if n == 1 else 0
-            cut = (352, 352, 704)[n]
-            rows = wo_raw[(n, g)]
-            grouped = wo_grouped[g][:, first : first + width]
-            regroup(nc.vector.tensor_copy, grouped[:, 0:cut], rows[:, :, 0:cut])
-            if 0:
-                for n0 in range(cut, width, TURN_COLS):
-                    nc.scalar.copy(out=grouped[:, n0 : n0 + TURN_COLS], in_=turn(rows, n0)[:])
-            elif cut < width:
-                regroup(nc.scalar.copy, grouped[:, cut:width], rows[:, :, cut:width])
-
-        def quantise_out(g):
-            nc.vector.quantize_mx(
-                out=wo_codes[:, g].bitcast(FP8X4),
-                scales=wo_scales[:, g],
-                in_=wo_grouped[g][:].rearrange("p n t -> p (n t)"),
-            )
-
-        def turn_attn(m):
-            a_t = psum.tile([P, PASSES, 2, P], F32, tag=("gate", "up")[m % 2], name="a_t")
-            transpose_words(a_sb[:, m, :].bitcast(F32), a_t)
-            words_out(a_grouped[:, m, :], a_t)
-
-        def quantise_attn(m):
-            nc.vector.quantize_mx(
-                out=a_codes[:, m].rearrange("p g r -> p (g r)").bitcast(FP8X4),
-                scales=a_scales[:, m].rearrange("p g r -> p (g r)"),
-                in_=a_grouped[:, m, :],
-            )
-
-        h_sb = keep.tile([P, M_TILES, E], F32)
-        sumsq = keep.tile([P, M_TILES, 8], F32)
-        std = keep.tile([P, M_TILES, 8], F32)
-        rstd = keep.tile([P, M_TILES, 8], F32)
-        sums = keep.tile([P, M_TILES], F32)
-        roots = keep.tile([P, M_TILES], F32)
-        inverse = keep.tile([P, M_TILES], F32)
-        h_grouped = keep.tile([P, M_TILES, PASSES * P * PACK], BF16, align_bytes=64, tag="tokens")
+        hn_grouped = keep.tile([P, M_TILES, PASSES * P * PACK], BF16, align_bytes=64)
         hn_codes = keep.tile([P, M_TILES, PASSES, P], U32, align_bytes=64)
         hn_scales = keep.tile([P, M_TILES, PASSES, P], U8, align_bytes=64)
-
-        acc_of = {}
-        hn_of = {}
-        def project(m, n):
-            acc = psum.tile([P, N_TILE], F32, tag=("gate", "up")[m % 2], name="acc")
-            for g in range(PASSES):
-                nc.tensor.matmul_mx(
-                    out=acc[:],
-                    lhsT=a_codes[:, m, g, :].bitcast(FP8X4),
-                    lhsT_scale=a_scales[:, m, g, :],
-                    rhs=wo_codes[:, g, n * H : (n + 1) * H].bitcast(FP8X4),
-                    rhs_scale=wo_scales[:, g, n * H : (n + 1) * H],
-                    start=(g == 0),
-                    stop=(g == PASSES - 1),
-                )
-            acc_of[(m, n)] = acc
-
-        def add(m, n):
-            cols = slice(n * N_TILE, (n + 1) * N_TILE)
-            nc.vector.tensor_tensor(out=h_sb[:, m, cols], in0=acc_of[(m, n)][:], in1=x_sb[:, m, cols], op=ALU.add)
-
-        def square(m):
-            squares = work.tile([P, E], BF16, tag="squares", name="squares", bufs=2)
-            nc.scalar.activation(out=squares[:], in_=h_sb[:, m, :], func=ACT.Square, accum_out=sumsq[:, m, 0:1])
-            nc.scalar.activation(out=std[:, m, 0:1], in_=sumsq[:, m, 0:1], func=ACT.Sqrt, scale=1.0 / E, bias=eps[:, 0:1])
-
-        def square_only(m):
-            squares = work.tile([P, E], BF16, tag="squares", name="squares", bufs=2)
-            nc.scalar.activation(out=squares[:], in_=h_sb[:, m, :], func=ACT.Square, accum_out=sums[:, m : m + 1])
-
-        def root_all():
-            nc.scalar.activation(out=roots[:], in_=sums[:], func=ACT.Sqrt, scale=1.0 / E, bias=eps[:, 0:1])
-
-        def root_pair(k):
-            two = slice(2 * k, 2 * k + 2)
-            nc.scalar.activation(out=roots[:, two], in_=sums[:, two], func=ACT.Sqrt, scale=1.0 / E, bias=eps[:, 0:1])
-
-        def reciprocal_pair(k):
-            two = slice(2 * k, 2 * k + 2)
-            nc.vector.reciprocal(out=inverse[:, two], in_=roots[:, two])
-
-        def power_pair(k):
-            two = slice(2 * k, 2 * k + 2)
-            nc.gpsimd.tensor_scalar(
-                out=roots[:, two], in0=sums[:, two], scalar1=1.0 / E, scalar2=EPS, op0=ALU.mult, op1=ALU.add
-            )
-            nc.gpsimd.tensor_tensor(out=inverse[:, two], in0=roots[:, two], in1=minus_half[:, two], op=ALU.pow)
-
-        def power_all():
-            nc.gpsimd.tensor_scalar(
-                out=roots[:], in0=sums[:], scalar1=1.0 / E, scalar2=EPS, op0=ALU.mult, op1=ALU.add
-            )
-            nc.gpsimd.tensor_tensor(out=inverse[:], in0=roots[:], in1=minus_half[:], op=ALU.pow)
-
-        def reciprocal_all():
-            nc.vector.reciprocal(out=inverse[:], in_=roots[:])
-
-        def norm_only(m):
-            hn = work.tile([P, E], BF16, tag="hn", name="hn", bufs=2)
-            for n in range(2) if 0 else range(1):
-                cols = slice(n * N_TILE, (n + 1) * N_TILE) if 0 else slice(0, E)
-                nc.vector.scalar_tensor_tensor(
-                    out=hn[:, cols], in0=h_sb[:, m, cols], scalar=inverse[:, m : m + 1],
-                    in1=gain_of[n][:] if 0 else gain[:], op0=ALU.mult, op1=ALU.mult
-                )
-            hn_of[m] = hn
-
-        def store_h(m):
-            nc.sync.dma_start(out=h_rows[:, m, :], in_=h_sb[:, m, :])
-
-        def norm(m):
-            nc.vector.reciprocal(out=rstd[:, m, 0:1], in_=std[:, m, 0:1])
-            hn = work.tile([P, E], BF16, tag="hn", name="hn", bufs=2)
+        interleave_vector(0)
+        interleave_scalar(0)
+        for m in range(M_TILES):
+            if m == 2:
+                interleave_scalar(1)
+            hn = work.tile([P, E], BF16, tag="hn", name="hn")
             nc.vector.scalar_tensor_tensor(
-                out=hn[:], in0=h_sb[:, m, :], scalar=rstd[:, m, 0:1], in1=gain[:], op0=ALU.mult, op1=ALU.mult
+                out=hn[:], in0=h_sb[:, m, :], scalar=rstd[:, m : m + 1], in1=gain[:], op0=ALU.mult, op1=ALU.mult
             )
-            hn_of[m] = hn
+            transpose_tokens(hn[:], hn_grouped[:, m, :], m)
+        interleave_vector(1)
+        quantise_unit(0)
+        for m in range(M_TILES):
+            quantise_tokens(hn_grouped, hn_codes, hn_scales, m)
 
-        def turn_norm(m):
-            hn_t = psum.tile([P, PASSES, 2, P], F32, tag=("gate", "up")[m % 2], name="hn_t")
-            transpose_words(hn_of[m][:].bitcast(F32), hn_t)
-            words_out(h_grouped[:, m, :], hn_t)
+        jobs_of = []
+        for c, width in enumerate(WIDTHS):
+            tiles = 1 if c == len(WIDTHS) - 1 else N_TILE // width
+            jobs_of.append([(c, m, tiles) for m in range(0, M_TILES, tiles)])
+        jobs_in_step = {}
+        for c, jobs in enumerate(jobs_of):
+            half = (len(jobs) + 1) // 2
+            jobs_in_step[PASSES * (c + 1)] = jobs[:half]
+            jobs_in_step[PASSES * (c + 1) + 1] = jobs[half:]
+        banks_of = {}
+        gated_of = {}
 
-        def quantise_norm(m):
-            nc.vector.quantize_mx(
-                out=hn_codes[:, m].rearrange("p g r -> p (g r)").bitcast(FP8X4),
-                scales=hn_scales[:, m].rearrange("p g r -> p (g r)"),
-                in_=h_grouped[:, m, :],
-            )
-
-        jobs = []
-        for c, (col0, width) in enumerate(chunks):
-            per = N_TILE // width if not (1 and c == len(chunks) - 1) else 1
-            for m0 in range(0, M_TILES, per):
-                jobs.append((c, m0, per))
-
-        def multiply(r):
-            c, m0, per = jobs[r]
-            width = chunks[c][1]
-            acc = [psum.tile([P, per, width], F32, tag=tag, name="acc2") for tag in ("gate", "up")]
-            banks_of[r] = acc
+        def multiply(job):
+            c, first, tiles = job
+            acc_gate = psum.tile([P, tiles, WIDTHS[c]], F32, tag="gate", name="acc_gate")
+            acc_up = psum.tile([P, tiles, WIDTHS[c]], F32, tag="up", name="acc_up")
+            banks_of[job] = (acc_gate, acc_up)
             w_codes, w_scales = codes_of[c]
             for w in range(2):
-                for k in range(per):
+                for k in range(tiles):
                     for g in range(PASSES):
                         nc.tensor.matmul_mx(
-                            out=acc[w][:, k, :],
-                            lhsT=hn_codes[:, m0 + k, g, :].bitcast(FP8X4),
-                            lhsT_scale=hn_scales[:, m0 + k, g, :],
+                            out=banks_of[job][w][:, k, :],
+                            lhsT=hn_codes[:, first + k, g, :].bitcast(FP8X4),
+                            lhsT_scale=hn_scales[:, first + k, g, :],
                             rhs=w_codes[:, g, w, :].bitcast(FP8X4),
                             rhs_scale=w_scales[:, g, w, :],
                             start=(g == 0),
                             stop=(g == PASSES - 1),
                         )
 
-        pair_of = {}
+        def gelu(job):
+            c, first, tiles = job
+            gated = work.tile([P, tiles, WIDTHS[c]], F32, tag="gated", name="gated", bufs=ACT_BUFS)
+            nc.scalar.activation(out=gated[:], in_=banks_of[job][0][:], func=ACT.Gelu_apprx_tanh)
+            gated_of[job] = gated
 
-        def gelu(r):
-            c, m0, per = jobs[r]
-            width = chunks[c][1]
-            if 0 and width == N_TILE and c < 0:
-                if c % 2 == 0:
-                    pair_of[m0] = work.tile([P, 2, N_TILE], F32, tag="gated2", name="gated2", bufs=12 // 2)
-                gated = pair_of[m0][:, c % 2]
-            else:
-                single = work.tile([P, per, width], F32, tag="gated", name="gated", bufs=12 if not 0 else 6)
-                gated = single[:]
-            nc.scalar.activation(out=gated, in_=banks_of[r][0][:] if per > 1 else banks_of[r][0][:, 0, :], func=ACT.Gelu_apprx_tanh) if 0 and width == N_TILE and c < 0 else nc.scalar.activation(out=gated, in_=banks_of[r][0][:], func=ACT.Gelu_apprx_tanh)
-            gated_of[r] = gated
+        def product(job):
+            c, first, tiles = job
+            gated = gated_of[job]
+            nc.vector.tensor_tensor(out=gated[:], in0=banks_of[job][1][:], in1=gated[:], op=ALU.mult)
+            cols = slice(first_cols[c], first_cols[c] + WIDTHS[c])
+            nc.sync.dma_start(out=act_tokens[:, first : first + tiles, cols], in_=gated[:])
 
-        def product(r):
-            c, m0, per = jobs[r]
-            col0, width = chunks[c]
-            gated = gated_of[r]
-            paired = 0 and width == N_TILE and c < 0
-            bank = banks_of[r][1][:, 0, :] if paired else banks_of[r][1][:]
-            nc.vector.tensor_tensor(out=gated, in0=bank, in1=gated, op=ALU.mult)
-            if not paired:
-                nc.sync.dma_start(out=act_rows[:, m0 : m0 + per, col0 : col0 + width], in_=gated)
-            elif c % 2:
-                nc.sync.dma_start(
-                    out=act_rows[:, m0, col0 - N_TILE : col0 + N_TILE], in_=pair_of[m0][:].rearrange("p c n -> p (c n)")
-                )
-
-        order = ([0, 1, 2, 3] if 0 else [0, 1, 3, 2]) + list(range(4, LOADS))
-        loads_done = []
-
-        def load_next():
-            if len(loads_done) < LOADS:
-                load_weights(order[len(loads_done)])
-                loads_done.append(1)
-
-        load_out(0, 0)
-        load_out(1, 0)
-        load_out(2, 1)
-        load_attn(0)
-        load_attn(2)
-        load_gain()
-        load_x(0)
-        load_x(2)
-        load_next()
-        load_next()
-        load_next()
-        load_next()
-        load_next()
-        load_next()
-        regroup_out(0, 0)
-        regroup_out(1, 0)
-        quantise_out(0)
-        regroup_out(2, 1)
-        turn_attn(0)
-        turn_attn(1)
-        turn_attn(2)
-        turn_attn(3)
-        quantise_out(1)
-        quantise_attn(0)
-        quantise_attn(1)
-        quantise_attn(2)
-        quantise_attn(3)
-        spread_gain()
-        load_next()
-        load_next()
-        load_next()
-        project(0, 0)
-        project(0, 1)
-        add(0, 0)
-        add(0, 1)
-        square_only(0)
-        project(1, 0)
-        project(1, 1)
-        add(1, 0)
-        add(1, 1)
-        square_only(1)
-        power_pair(0)
-        project(2, 0)
-        project(2, 1)
-        add(2, 0)
-        add(2, 1)
-        square_only(2)
-        project(3, 0)
-        project(3, 1)
-        add(3, 0)
-        add(3, 1)
-        square_only(3)
-        power_pair(1)
-        regroup_vector(0)
-        regroup_scalar(0)
-        norm_only(0)
-        turn_norm(0)
-        norm_only(1)
-        turn_norm(1)
-        open_unit(1)
-        regroup_scalar(1)
-        norm_only(2)
-        turn_norm(2)
-        norm_only(3)
-        turn_norm(3)
-        regroup_vector(1)
-        quantise_unit(0)
-        quantise_norm(0)
-        quantise_norm(1)
-        quantise_norm(2)
-        quantise_norm(3)
-
-        mult = {}
-        for c in range(len(chunks)):
-            mine = [r for r in range(len(jobs)) if jobs[r][0] == c]
-            half = -(-len(mine) // 2)
-            mult[2 * c + 2] = mine[:half]
-            mult[2 * c + 3] = mine[half:]
-        nu = len(units)
-        for i in range(2, nu + 4):
-            if i < nu:
-                regroup_vector(i)
-            if i <= nu:
+        for i in range(WHOLE_GATE_UNITS, UNITS + 4):
+            if i < UNITS:
+                interleave_vector(i)
+            if i <= UNITS:
                 quantise_unit(i - 1)
-            load_next()
-            for r in mult.get(i - 2, []):
-                product(r)
-            if 9 <= i < 13:
-                store_h(i - 9)
-            if i + 1 < nu:
-                regroup_gps(i + 1)
-            if i < nu:
-                copy_turned(i)
-            if i < nu:
-                regroup_scalar(i)
-            if i + 1 < nu:
-                turn_unit(i + 1)
-            for r in mult.get(i, []):
-                multiply(r)
-            for r in mult.get(i - 1, []):
-                gelu(r)
+            if RAW_BUFS + i - 2 < LOADS:
+                load_weights(RAW_BUFS + i - 2)
+            for job in jobs_in_step.get(i - 2, []):
+                product(job)
+            if H_STORES <= i < H_STORES + M_TILES:
+                m = i - H_STORES
+                nc.sync.dma_start(out=h_tokens[:, m, :], in_=h_sb[:, m, :])
+            if FIRST_GPSIMD_UNIT <= i + 1 < UNITS:
+                interleave_gpsimd(i + 1)
+            if i < UNITS:
+                interleave_scalar(i)
+            for job in jobs_in_step.get(i, []):
+                multiply(job)
+            for job in jobs_in_step.get(i - 1, []):
+                gelu(job)

from contextlib import ExitStack

import concourse.mybir as mybir
from concourse.masks import make_identity

F32 = mybir.dt.float32
BF16 = mybir.dt.bfloat16
U32 = mybir.dt.uint32
U8 = mybir.dt.uint8
FP8X4 = mybir.dt.float8_e4m3fn_x4
ACT = mybir.ActivationFunctionType
ALU = mybir.AluOpType

P = 128
PACK = 4
K_PASS = P * PACK
TOKENS = 512
M_TILES = TOKENS // P
E = 1024
F = 4096
PASSES = E // K_PASS
N_TILE = 512
HALF = E // 2
EPS = 1e-6

LOAD_COLS = 1024
LOADS = 2 * PASSES * (F // LOAD_COLS)
FIRST_LOADS = (0, 1, 3, 2)

WIDTHS = (512,) * 7 + (256, 256)
UNITS = len(WIDTHS) * PASSES

OUT_VECTOR_COLS = {HALF: 352, E: 704}
GATE_VECTOR_COLS = {512: 408, 256: 168}
WHOLE_GATE_UNITS = 2
UP_VECTOR_COLS = 96
UP_VECTOR_UNITS = (3, 4)
UP_GPSIMD_COLS = 128
FIRST_GPSIMD_UNIT = 5
H_STORES = 9

RAW_BUFS = 9
ACT_BUFS = 12

FLOPS = 2 * TOKENS * E * (E + 2 * F)


def interleave(copy, grouped, rows):
    copy(
        out=grouped.rearrange("p (c i) t -> p c t i", i=4),
        in_=rows.rearrange("p t (c i) -> p c t i", i=4),
    )


def tile_block_pb_kernel(tc, attn, x, w_out, scale2, w_gate, w_up, out_0, out_1):
    nc = tc.nc
    attn_tokens = attn.rearrange("b s i d -> (b s) (i d)").rearrange("(p m) k -> p m k", p=P)
    x_tokens = x.rearrange("b s e -> (b s) e").rearrange("(p m) e -> p m e", p=P)
    h_tokens = out_0.rearrange("b s e -> (b s) e").rearrange("(p m) e -> p m e", p=P)
    act_tokens = out_1.rearrange("b s f -> (b s) f").rearrange("(p m) f -> p m f", p=P)
    w_out_rows = w_out.rearrange("i d e -> (i d) e").rearrange("(g p t) n -> g p t n", t=PACK, p=P)
    gate_up_rows = [w.rearrange("(g p t) n -> g p t n", t=PACK, p=P) for w in (w_gate, w_up)]

    with ExitStack() as ctx:
        const = ctx.enter_context(tc.tile_pool(name="const", bufs=1))
        keep = ctx.enter_context(tc.tile_pool(name="keep", bufs=1))
        raw_pool = ctx.enter_context(tc.tile_pool(name="raw", bufs=RAW_BUFS))
        grouped_pool = ctx.enter_context(tc.tile_pool(name="grouped", bufs=2))
        code_pool = ctx.enter_context(tc.tile_pool(name="codes", bufs=3))
        work = ctx.enter_context(tc.tile_pool(name="work", bufs=2))
        psum = ctx.enter_context(tc.psum_pool(name="psum", bufs=4))
        ctx.enter_context(tc.manual_schedule())

        ident = const.tile([P, P], F32)
        make_identity(nc, ident[:])
        gain_row = const.tile([P, E], BF16)
        nc.gpsimd.memset(gain_row[:], 0.0)
        minus_half = const.tile([P, M_TILES], F32)
        nc.gpsimd.memset(minus_half[:], -0.5)
        ones = const.tile([P, P], BF16)
        nc.vector.memset(ones[:], 1.0)
        warm = const.tile([P, 1], F32)
        nc.scalar.activation(out=warm[:], in_=ones[:, 0:1], func=ACT.Gelu_apprx_tanh)

        w_out_raw = {}

        def load_w_out(g, first, width):
            raw = raw_pool.tile([P, PACK, width], BF16, tag="raw", name="raw_o")
            nc.sync.dma_start(out=raw[:], in_=w_out_rows[g][:, :, first : first + width])
            w_out_raw[(g, first)] = raw

        gate_up_raw = {}
        load_order = FIRST_LOADS + tuple(range(len(FIRST_LOADS), LOADS))

        def load_weights(k):
            q, rest = divmod(load_order[k], 2 * PASSES)
            g, w = divmod(rest, 2)
            raw = raw_pool.tile([P, PACK, LOAD_COLS], BF16, tag="raw", name="raw_w")
            nc.sync.dma_start(out=raw[:], in_=gate_up_rows[w][g][:, :, q * LOAD_COLS : (q + 1) * LOAD_COLS])
            gate_up_raw[(w, g, q)] = raw

        load_w_out(0, 0, HALF)
        load_w_out(0, HALF, HALF)
        load_w_out(1, 0, E)
        attn_sb = keep.tile([P, M_TILES, E], BF16)
        for m in range(0, M_TILES, 2):
            nc.sync.dma_start(out=attn_sb[:, m : m + 2, :], in_=attn_tokens[:, m : m + 2, :])
        nc.sync.dma_start(out=gain_row[0:1, :], in_=scale2.unsqueeze(0))
        x_sb = keep.tile([P, M_TILES, E], BF16)
        for m in range(0, M_TILES, 2):
            nc.sync.dma_start(out=x_sb[:, m : m + 2, :], in_=x_tokens[:, m : m + 2, :])
        free_bufs = RAW_BUFS - len(w_out_raw)
        for k in range(free_bufs):
            load_weights(k)

        w_out_codes = keep.tile([P, PASSES, E], U32, align_bytes=64)
        w_out_scales = keep.tile([P, PASSES, E], U8, align_bytes=64)
        w_out_grouped = {}

        def interleave_w_out(g, first, width):
            if first == 0:
                w_out_grouped[g] = grouped_pool.tile([P, E, PACK], BF16, align_bytes=64, tag="grouped", name="grouped")
            grouped = w_out_grouped[g][:, first : first + width]
            rows = w_out_raw[(g, first)]
            cut = OUT_VECTOR_COLS[width]
            interleave(nc.vector.tensor_copy, grouped[:, 0:cut], rows[:, :, 0:cut])
            interleave(nc.scalar.copy, grouped[:, cut:width], rows[:, :, cut:width])

        def quantise_w_out(g):
            nc.vector.quantize_mx(
                out=w_out_codes[:, g].bitcast(FP8X4),
                scales=w_out_scales[:, g],
                in_=w_out_grouped[g][:].rearrange("p n t -> p (n t)"),
            )

        def transpose_tokens(values, grouped, m):
            words = values.bitcast(F32)
            words_t = psum.tile([P, PASSES, 2, P], F32, tag=("gate", "up")[m % 2], name="words_t")
            for g in range(PASSES):
                for v in range(2):
                    first = 2 * g * P + v
                    nc.tensor.transpose(words_t[:, g, v, :], words[:, first : 2 * (g + 1) * P : 2], ident[:])
            nc.scalar.copy(
                out=grouped.bitcast(F32).rearrange("p (g r v) -> p g r v", g=PASSES, v=2),
                in_=words_t[:].rearrange("p g v r -> p g r v"),
            )

        def quantise_tokens(grouped, codes, scales, m):
            nc.vector.quantize_mx(
                out=codes[:, m].rearrange("p g r -> p (g r)").bitcast(FP8X4),
                scales=scales[:, m].rearrange("p g r -> p (g r)"),
                in_=grouped[:, m, :],
            )

        attn_grouped = keep.tile([P, M_TILES, PASSES * P * PACK], BF16, align_bytes=64)
        attn_codes = keep.tile([P, M_TILES, PASSES, P], U32, align_bytes=64)
        attn_scales = keep.tile([P, M_TILES, PASSES, P], U8, align_bytes=64)

        interleave_w_out(0, 0, HALF)
        interleave_w_out(0, HALF, HALF)
        quantise_w_out(0)
        interleave_w_out(1, 0, E)
        for m in range(M_TILES):
            transpose_tokens(attn_sb[:, m, :], attn_grouped[:, m, :], m)
        quantise_w_out(1)
        for m in range(M_TILES):
            quantise_tokens(attn_grouped, attn_codes, attn_scales, m)

        gain = const.tile([P, E], F32)
        for n in range(E // N_TILE):
            cols = slice(n * N_TILE, (n + 1) * N_TILE)
            spread = psum.tile([P, N_TILE], F32, tag=("gate", "up")[n], name="spread")
            nc.tensor.matmul(out=spread[:], lhsT=ones[:], rhs=gain_row[:, cols], start=True, stop=True)
            nc.scalar.copy(out=gain[:, cols], in_=spread[:])
        for k in range(free_bufs, RAW_BUFS):
            load_weights(k)

        first_cols = [sum(WIDTHS[:c]) for c in range(len(WIDTHS))]
        grouped_of = {}
        codes_of = {}

        def unit_rows(u, w):
            c, g = divmod(u, PASSES)
            q, first = divmod(first_cols[c], LOAD_COLS)
            return gate_up_raw[(w, g, q)][:, :, first : first + WIDTHS[c]]

        def unit_grouped(u):
            if u not in grouped_of:
                width = WIDTHS[u // PASSES]
                grouped_of[u] = grouped_pool.tile(
                    [P, 2, width, PACK], BF16, align_bytes=64, tag="grouped", name="grouped"
                )
            return grouped_of[u]

        def gate_cut(u):
            width = WIDTHS[u // PASSES]
            return width if u < WHOLE_GATE_UNITS else GATE_VECTOR_COLS[width]

        def up_cut(u):
            width = WIDTHS[u // PASSES]
            if u in UP_VECTOR_UNITS:
                return width - UP_VECTOR_COLS
            return width - UP_GPSIMD_COLS if u >= FIRST_GPSIMD_UNIT else width

        def interleave_vector(u):
            grouped = unit_grouped(u)
            interleave(nc.vector.tensor_copy, grouped[:, 0, 0 : gate_cut(u)], unit_rows(u, 0)[:, :, 0 : gate_cut(u)])
            if u in UP_VECTOR_UNITS:
                interleave(nc.vector.tensor_copy, grouped[:, 1, up_cut(u) :], unit_rows(u, 1)[:, :, up_cut(u) :])

        def interleave_scalar(u):
            grouped = unit_grouped(u)
            interleave(nc.scalar.copy, grouped[:, 1, 0 : up_cut(u)], unit_rows(u, 1)[:, :, 0 : up_cut(u)])
            if gate_cut(u) < WIDTHS[u // PASSES]:
                interleave(nc.scalar.copy, grouped[:, 0, gate_cut(u) :], unit_rows(u, 0)[:, :, gate_cut(u) :])

        def interleave_gpsimd(u):
            nc.gpsimd.tensor_scalar(
                out=unit_grouped(u)[:, 1, up_cut(u) :, :],
                in0=unit_rows(u, 1)[:, :, up_cut(u) :].rearrange("p t n -> p n t"),
                scalar1=1.0,
                scalar2=0.0,
                op0=ALU.mult,
                op1=ALU.add,
            )

        def quantise_unit(u):
            c, g = divmod(u, PASSES)
            if g == 0:
                shape = [P, PASSES, 2, WIDTHS[c]]
                w_codes = code_pool.tile(shape, U32, align_bytes=64, tag="w_codes", name="w_codes")
                w_scales = code_pool.tile(shape, U8, align_bytes=64, tag="w_scales", name="w_scales")
                codes_of[c] = (w_codes, w_scales)
            w_codes, w_scales = codes_of[c]
            nc.vector.quantize_mx(
                out=w_codes[:, g].rearrange("p w n -> p (w n)").bitcast(FP8X4),
                scales=w_scales[:, g].rearrange("p w n -> p (w n)"),
                in_=grouped_of[u][:].rearrange("p w n t -> p (w n t)"),
            )

        h_sb = keep.tile([P, M_TILES, E], F32)
        sums = keep.tile([P, M_TILES], F32)
        means = keep.tile([P, M_TILES], F32)
        rstd = keep.tile([P, M_TILES], F32)
        for m in range(M_TILES):
            for n in range(E // N_TILE):
                cols = slice(n * N_TILE, (n + 1) * N_TILE)
                acc = psum.tile([P, N_TILE], F32, tag=("gate", "up")[m % 2], name="acc")
                for g in range(PASSES):
                    nc.tensor.matmul_mx(
                        out=acc[:],
                        lhsT=attn_codes[:, m, g, :].bitcast(FP8X4),
                        lhsT_scale=attn_scales[:, m, g, :],
                        rhs=w_out_codes[:, g, cols].bitcast(FP8X4),
                        rhs_scale=w_out_scales[:, g, cols],
                        start=(g == 0),
                        stop=(g == PASSES - 1),
                    )
                nc.vector.tensor_tensor(out=h_sb[:, m, cols], in0=acc[:], in1=x_sb[:, m, cols], op=ALU.add)
            squares = work.tile([P, E], BF16, tag="squares", name="squares")
            nc.scalar.activation(out=squares[:], in_=h_sb[:, m, :], func=ACT.Square, accum_out=sums[:, m : m + 1])
            if m % 2 == 1:
                two = slice(m - 1, m + 1)
                nc.gpsimd.tensor_scalar(
                    out=means[:, two], in0=sums[:, two], scalar1=1.0 / E, scalar2=EPS, op0=ALU.mult, op1=ALU.add
                )
                nc.gpsimd.tensor_tensor(out=rstd[:, two], in0=means[:, two], in1=minus_half[:, two], op=ALU.pow)

        hn_grouped = keep.tile([P, M_TILES, PASSES * P * PACK], BF16, align_bytes=64)
        hn_codes = keep.tile([P, M_TILES, PASSES, P], U32, align_bytes=64)
        hn_scales = keep.tile([P, M_TILES, PASSES, P], U8, align_bytes=64)
        interleave_vector(0)
        interleave_scalar(0)
        for m in range(M_TILES):
            if m == 2:
                interleave_scalar(1)
            hn = work.tile([P, E], BF16, tag="hn", name="hn")
            nc.vector.scalar_tensor_tensor(
                out=hn[:], in0=h_sb[:, m, :], scalar=rstd[:, m : m + 1], in1=gain[:], op0=ALU.mult, op1=ALU.mult
            )
            transpose_tokens(hn[:], hn_grouped[:, m, :], m)
        interleave_vector(1)
        quantise_unit(0)
        for m in range(M_TILES):
            quantise_tokens(hn_grouped, hn_codes, hn_scales, m)

        jobs_of = []
        for c, width in enumerate(WIDTHS):
            tiles = 1 if c == len(WIDTHS) - 1 else N_TILE // width
            jobs_of.append([(c, m, tiles) for m in range(0, M_TILES, tiles)])
        jobs_in_step = {}
        for c, jobs in enumerate(jobs_of):
            half = (len(jobs) + 1) // 2
            jobs_in_step[PASSES * (c + 1)] = jobs[:half]
            jobs_in_step[PASSES * (c + 1) + 1] = jobs[half:]
        banks_of = {}
        gated_of = {}

        def multiply(job):
            c, first, tiles = job
            acc_gate = psum.tile([P, tiles, WIDTHS[c]], F32, tag="gate", name="acc_gate")
            acc_up = psum.tile([P, tiles, WIDTHS[c]], F32, tag="up", name="acc_up")
            banks_of[job] = (acc_gate, acc_up)
            w_codes, w_scales = codes_of[c]
            for w in range(2):
                for k in range(tiles):
                    for g in range(PASSES):
                        nc.tensor.matmul_mx(
                            out=banks_of[job][w][:, k, :],
                            lhsT=hn_codes[:, first + k, g, :].bitcast(FP8X4),
                            lhsT_scale=hn_scales[:, first + k, g, :],
                            rhs=w_codes[:, g, w, :].bitcast(FP8X4),
                            rhs_scale=w_scales[:, g, w, :],
                            start=(g == 0),
                            stop=(g == PASSES - 1),
                        )

        def gelu(job):
            c, first, tiles = job
            gated = work.tile([P, tiles, WIDTHS[c]], F32, tag="gated", name="gated", bufs=ACT_BUFS)
            nc.scalar.activation(out=gated[:], in_=banks_of[job][0][:], func=ACT.Gelu_apprx_tanh)
            gated_of[job] = gated

        def product(job):
            c, first, tiles = job
            gated = gated_of[job]
            nc.vector.tensor_tensor(out=gated[:], in0=banks_of[job][1][:], in1=gated[:], op=ALU.mult)
            cols = slice(first_cols[c], first_cols[c] + WIDTHS[c])
            nc.sync.dma_start(out=act_tokens[:, first : first + tiles, cols], in_=gated[:])

        for i in range(WHOLE_GATE_UNITS, UNITS + 4):
            if i < UNITS:
                interleave_vector(i)
            if i <= UNITS:
                quantise_unit(i - 1)
            if RAW_BUFS + i - 2 < LOADS:
                load_weights(RAW_BUFS + i - 2)
            for job in jobs_in_step.get(i - 2, []):
                product(job)
            if H_STORES <= i < H_STORES + M_TILES:
                m = i - H_STORES
                nc.sync.dma_start(out=h_tokens[:, m, :], in_=h_sb[:, m, :])
            if FIRST_GPSIMD_UNIT <= i + 1 < UNITS:
                interleave_gpsimd(i + 1)
            if i < UNITS:
                interleave_scalar(i)
            for job in jobs_in_step.get(i, []):
                multiply(job)
            for job in jobs_in_step.get(i - 1, []):
                gelu(job)
